import numpy as np
import ml_dtypes


def mxq(x, axis, fmt="e4m3"):
    dtype, down = {"e4m3": (ml_dtypes.float8_e4m3fn, 7), "e5m2": (ml_dtypes.float8_e5m2, 14)}[fmt]
    v = np.moveaxis(np.asarray(x, np.float32).astype(ml_dtypes.bfloat16).astype(np.float64), axis, -1)
    blocks = v.reshape(v.shape[:-1] + (-1, 32))
    amax = np.abs(blocks).max(-1, keepdims=True)
    byte = np.maximum(np.where(amax > 0, np.frexp(amax)[1] - 1 + 127, 0) - down, 1)
    scale = np.exp2(byte - 127.0)
    codes = (blocks / scale).astype(np.float32).astype(dtype).astype(np.float64)
    return np.moveaxis((codes * scale).reshape(v.shape), -1, axis)


WIDE = False


def mx_kscale(k):
    if not WIDE:
        return np.ones(k)
    levels = np.array([10, -10, 5, -5, 0])
    if k % 512:
        return np.exp2(np.random.permutation(np.resize(levels, k // 32))).repeat(32)
    a = np.empty((k // 512, 16))
    for p in range(k // 512):
        a[p, :8] = np.random.permutation(np.resize(levels, 8))
        for g in range(8):
            far = levels[np.abs(levels - a[p, g]) >= 10]
            a[p, g + 8] = far[np.random.randint(len(far))]
    return np.exp2(a.ravel()).repeat(32)


BF16 = ml_dtypes.bfloat16


def bf(x):
    return np.asarray(x, np.float32).astype(BF16)


def f64(x):
    return np.asarray(x).astype(np.float64)


B, S, D, H, HD, W = 1, 2048, 1024, 8, 128, 256
E = H * HD
HALF = HD // 2


def rope(t, cos, sin):
    tr = t.reshape(t.shape[:-1] + (HALF, 2))
    r, i = tr[..., 0], tr[..., 1]
    c = cos[None, :, None, :]
    s = sin[None, :, None, :]
    return np.stack([r * c - i * s, r * s + i * c], axis=-1).reshape(t.shape)


def draw0():
    s = mx_kscale(D)
    ang = np.outer(np.arange(S), 1.0 / 10000.0 ** (np.arange(0, HD, 2) / HD))
    return {"x": bf(np.random.standard_normal((B, S, D)) * s),
            "freqs_cos": bf(np.cos(ang)), "freqs_sin": bf(np.sin(ang)),
            "wq": bf(np.random.standard_normal((E, D)) * 1.25 / np.sqrt(D) / s[None, :]),
            "wk": bf(np.random.standard_normal((E, D)) * 1.25 / np.sqrt(D) / s[None, :])}


def core(x, freqs_cos, freqs_sin, wq, wk):
    xm = mxq(f64(x), 2, "e4m3")
    q = (xm @ mxq(f64(wq), 1, "e4m3").T).reshape(B, S, H, HD)
    k = (xm @ mxq(f64(wk), 1, "e4m3").T).reshape(B, S, H, HD)
    q = rope(q, f64(freqs_cos), f64(freqs_sin))
    k = rope(k, f64(freqs_cos), f64(freqs_sin))
    return q.transpose(0, 2, 1, 3), k.transpose(0, 2, 1, 3)


def e4m3fn_bytes(y):
    return np.clip(np.asarray(y, np.float64), -448.0, 448.0).astype(np.float32).astype(ml_dtypes.float8_e4m3fn).view(np.uint8)


def e4m3fn_values(b):
    return np.asarray(b, np.uint8).view(ml_dtypes.float8_e4m3fn).astype(np.float64)


def setup_inputs():
    d = draw0()
    x0 = np.asarray(d['x']).astype(np.float64)
    s = (np.max(np.abs(x0), axis=(0, 1), keepdims=True) / 448.0).astype(np.float32)
    out = {}
    for k, v in d.items():
        if k == 'x':
            out['x_bytes'] = e4m3fn_bytes(x0 / s.astype(np.float64))
            out['x_scale'] = s
        else:
            out[k] = v
    return out


def reference(x_bytes, x_scale, freqs_cos, freqs_sin, wq, wk):
    return core(e4m3fn_values(x_bytes) * x_scale.astype(np.float64), freqs_cos, freqs_sin, wq, wk)

@@ -1,0 +1,325 @@
+from contextlib import ExitStack
+
+import concourse.mybir as mybir
+from concourse.masks import make_identity
+
+FLOPS = 2 * 2048 * 2048 * 1024
+
+F32 = mybir.dt.float32
+BF16 = mybir.dt.bfloat16
+U32 = mybir.dt.uint32
+U8 = mybir.dt.uint8
+FP8 = mybir.dt.float8_e4m3fn
+FP8X4 = mybir.dt.float8_e4m3fn_x4
+ALU = mybir.AluOpType
+ACT = mybir.ActivationFunctionType
+
+P = 128
+D = 1024
+NT = 16
+NH = 16
+NB = 4
+NG = 2
+A_FB = (0, 1)
+B_FB = (2, 3)
+AV_FB = 3
+TP_TAGS = ("acc", "pt", "ob", "acc", "pt", "ob", "acc", "acc")
+TAG_BUFS = {"acc": 4, "pt": 2, "ob": 2}
+X_BEFORE_W = {3: 1, 8: 2, 13: 3}
+GROUPS = (2, 2, 2, 2, 2, 2, 1, 1, 1, 1)
+
+
+def tile_attention_pa_kernel(tc, x_bytes, x_scale, freqs_cos, freqs_sin, wq, wk, out_0, out_1):
+    nc = tc.nc
+    with ExitStack() as ctx:
+        ctx.enter_context(tc.manual_schedule())
+        const = ctx.enter_context(tc.tile_pool(name="const", bufs=1))
+        psum = ctx.enter_context(tc.psum_pool(name="psum", bufs=2))
+        counters = {"tp": 0}
+
+        def bank(shape, dtype, tag):
+            return psum.tile(shape, dtype, name=tag, tag=tag, bufs=TAG_BUFS[tag])
+
+        def tp_bank(shape, dtype):
+            tag = TP_TAGS[counters["tp"] % 8]
+            counters["tp"] += 1
+            return bank(shape, dtype, tag)
+
+        scale_bc = const.tile([P, D], F32, name="scale_bc")
+        cosb = const.tile([P, NT, 64], BF16, name="cosb")
+        sgn = const.tile([P, 2, NT, 64], BF16, name="sgn")
+        tab2 = const.tile([P, NT, P], BF16, name="tab2")
+        cosf = const.tile([P, NT, 32], F32, name="cosf")
+        tabT = const.tile([P, NT * P], BF16, name="tabT")
+        cst = {}
+        sel_c = {}
+        sel_s = {}
+        for b in B_FB:
+            cst[b] = const.tile([P, 2, NT * P], BF16, name="cst%d" % b)
+            sel_c[b] = const.tile([P, P], BF16, name="selc%d" % b)
+            sel_s[b] = const.tile([P, P], BF16, name="sels%d" % b)
+        wc = const.tile([P, NG, NB * 512], U32, name="wc", align_bytes=64)
+        ws = const.tile([P, NG, NB * 512], U8, name="ws", align_bytes=64)
+        xc = const.tile([P, NG, NT * P], U32, name="xc", align_bytes=64)
+        xs = const.tile([P, NG, NT * P], U8, name="xs", align_bytes=64)
+        ident = const.tile([P, P], F32, name="ident")
+        identb = const.tile([P, P], BF16, name="identb")
+        perm_w = const.tile([P, P], F32, name="perm_w")
+        perm_a = const.tile([P, P], F32, name="perm_a")
+        perm_b = const.tile([P, P], F32, name="perm_b")
+
+        with ExitStack() as head:
+            xin = head.enter_context(tc.tile_pool(name="xin", bufs=1))
+            xwork = head.enter_context(tc.tile_pool(name="xwork", bufs=4))
+            wraw_pool = head.enter_context(tc.tile_pool(name="wraw", bufs=NH))
+            wgp = head.enter_context(tc.tile_pool(name="wgp", bufs=1))
+            xbytes = [xin.tile([P, 4, D], U8, name="xbytes%d" % c) for c in range(4)]
+            wg = [wgp.tile([P, NB, NH, 32, 2], F32, name="wg%d" % g, align_bytes=64) for g in range(NG)]
+            x_view = x_bytes.rearrange("o (p t) k -> (o p) t k", t=NT)
+            cos_view = freqs_cos.rearrange("(p t) j -> p t j", t=NT)
+            sin_view = freqs_sin.rearrange("(p t) j -> p t j", t=NT)
+            wraw = []
+            xbf = []
+            xg = []
+
+            nc.sync.dma_start(out=xbytes[0][:, 0:1, :], in_=x_view[:, 0:1, :])
+            nc.sync.dma_start(out=scale_bc[:], in_=x_scale.rearrange("a b k -> (a b k)").partition_broadcast(P))
+            nc.sync.dma_start(out=xbytes[0][:, 1:4, :], in_=x_view[:, 1:4, :])
+            for h in range(NH):
+                if h in X_BEFORE_W:
+                    c = X_BEFORE_W[h]
+                    nc.sync.dma_start(out=xbytes[c][:], in_=x_view[:, 4 * c : 4 * c + 4, :])
+                w = wq if h < 8 else wk
+                wr = wraw_pool.tile([P, D], BF16, name="wr", tag="wr")
+                nc.sync.dma_start(out=wr[:], in_=w[(h % 8) * P : (h % 8 + 1) * P, :])
+                wraw.append(wr)
+            nc.sync.dma_start(out=tab2[:, :, 0:64], in_=sin_view)
+            nc.sync.dma_start(out=tab2[:, :, 64:128], in_=cos_view)
+            nc.sync.dma_start(out=cosb[:], in_=cos_view)
+            nc.sync.dma_start(out=sgn[:, 1, :, :], in_=sin_view)
+
+            make_identity(nc, ident[:])
+            make_identity(nc, identb[:])
+            nc.vector.tensor_copy(
+                out=perm_w[:].rearrange("p (b e j) -> p b e j", b=NB, e=2),
+                in_=ident[:].rearrange("p (b j e) -> p b e j", b=NB, e=2),
+            )
+            nc.vector.tensor_copy(
+                out=perm_a[:].rearrange("p (b j e) -> p b j e", b=NB, e=2),
+                in_=ident[:].rearrange("p (b e j) -> p b j e", b=NB, e=2),
+            )
+            nc.vector.tensor_copy(
+                out=perm_b[:].rearrange("p (b j e) -> p b j e", b=NB, e=2),
+                in_=ident[:].rearrange("p (b e j) -> p b j e", b=NB, e=2)[:, :, :, ::-1],
+            )
+            for b in B_FB:
+                nc.vector.tensor_copy(
+                    out=sel_c[b][:].rearrange("p (x j) -> p x j", j=16),
+                    in_=identb[:, 64 + 16 * b : 64 + 16 * (b + 1)].unsqueeze(1).to_broadcast([P, 8, 16]),
+                )
+                sv = sel_s[b][:].rearrange("p (h e j) -> p h e j", h=4, e=2)
+                src = identb[:, 16 * b : 16 * (b + 1)].unsqueeze(1).to_broadcast([P, 4, 16])
+                nc.vector.tensor_copy(out=sv[:, :, 0, :], in_=src)
+                nc.vector.tensor_scalar(out=sv[:, :, 1, :], in0=src, scalar1=-1.0, scalar2=None, op0=ALU.mult)
+
+            def transposes(words, permutation):
+                tp = tp_bank([P, 4, P], F32)
+                for g in range(NG):
+                    for u in range(2):
+                        nc.tensor.transpose(tp[:, 2 * g + u, :], words[:, 256 * g + u : 256 * (g + 1) : 2], permutation[:])
+                return tp
+
+            def x_quant(c):
+                for g in range(NG):
+                    nc.vector.quantize_mx(
+                        out=xc[:, g, 512 * c : 512 * (c + 1)].bitcast(FP8X4),
+                        scales=xs[:, g, 512 * c : 512 * (c + 1)],
+                        in_=xg[c][:, g, :, :, :].rearrange("p a n u -> p (a n u)").bitcast(BF16),
+                    )
+
+            for t in range(NT):
+                xb = xwork.tile([P, D], BF16, name="xbf", tag="xbf", bufs=NT)
+                nc.vector.tensor_tensor(out=xb[:], in0=xbytes[t // 4][:, t % 4, :].bitcast(FP8), in1=scale_bc[:], op=ALU.mult)
+                xbf.append(xb)
+            for t in range(NT):
+                if t % 4 == 0:
+                    xg.append(xwork.tile([P, NG, 4, P, 2], F32, name="xg", tag="xg", align_bytes=64))
+                tp = transposes(xbf[t][:].bitcast(F32), ident)
+                nc.scalar.copy(out=xg[t // 4][:, :, t % 4, :, :], in_=tp[:].rearrange("p (g u) n -> p g n u", u=2))
+                tp = transposes(wraw[t][:].bitcast(F32), perm_w)
+                for g in range(NG):
+                    nc.scalar.copy(
+                        out=wg[g][:, :, t, :, :], in_=tp[:, 2 * g : 2 * g + 2, :].rearrange("p u (b r) -> p b r u", b=NB)
+                    )
+                if t in (3, 7, 11):
+                    x_quant(t // 4)
+            for c in range(4):
+                tpb = bank([P, 4, P], BF16, "ob")
+                for i in range(4):
+                    nc.tensor.transpose(tpb[:, i, :], tab2[:, 4 * c + i, :], identb[:])
+                nc.scalar.copy(out=tabT[:, 512 * c : 512 * (c + 1)], in_=tpb[:].rearrange("p i n -> p (i n)"))
+            for c in range(4):
+                for b in B_FB:
+                    pm = bank([P, 2, 512], BF16, "ob")
+                    for v, sel in enumerate((sel_c[b], sel_s[b])):
+                        nc.tensor.matmul(out=pm[:, v, :], lhsT=sel[:], rhs=tabT[:, 512 * c : 512 * (c + 1)], start=True, stop=True)
+                    nc.scalar.copy(out=cst[b][:, :, 512 * c : 512 * (c + 1)], in_=pm[:])
+            for b in B_FB + A_FB:
+                for g in range(NG):
+                    nc.vector.quantize_mx(
+                        out=wc[:, g, 512 * b : 512 * (b + 1)].bitcast(FP8X4),
+                        scales=ws[:, g, 512 * b : 512 * (b + 1)],
+                        in_=wg[g][:, b, :, :, :].rearrange("p h r u -> p (h r u)").bitcast(BF16),
+                    )
+            x_quant(3)
+            nc.scalar.copy(out=cosf[:], in_=cosb[:, :, 0:32])
+            nc.scalar.activation(out=sgn[:, 0, :, :], in_=sgn[:, 1, :, :], func=ACT.Copy, scale=-1.0)
+
+        mpool = ctx.enter_context(tc.tile_pool(name="mpool", bufs=4))
+        opool = ctx.enter_context(tc.tile_pool(name="opool", bufs=4))
+        out_views = (
+            out_0.rearrange("o h (p t) f -> p (o h) t f", t=NT),
+            out_1.rearrange("o h (p t) f -> p (o h) t f", t=NT),
+        )
+        group_of = {}
+        t0 = 0
+        for n_t in GROUPS:
+            for a in range(n_t):
+                group_of[t0 + a] = (t0, n_t)
+            t0 += n_t
+        ots = {}
+
+        def ot_slice(t, b, n_b):
+            first, n_t = group_of[t]
+            if first not in ots:
+                ots[first] = opool.tile([P, NH, n_t, P], F32, name="ot", tag="ot")
+            return ots[first][:, :, t - first, 32 * b : 32 * (b + n_b)]
+
+        def a_mx(t, b):
+            acc = bank([P, 512], F32, "acc")
+            for g in range(NG):
+                nc.tensor.matmul_mx(
+                    out=acc[:],
+                    lhsT=xc[:, g, P * t : P * (t + 1)].bitcast(FP8X4),
+                    lhsT_scale=xs[:, g, P * t : P * (t + 1)],
+                    rhs=wc[:, g, 512 * b : 512 * (b + 1)].bitcast(FP8X4),
+                    rhs_scale=ws[:, g, 512 * b : 512 * (b + 1)],
+                    start=(g == 0),
+                    stop=(g == NG - 1),
+                )
+            return acc
+
+        def a_m1(t, i, acc, m1):
+            b = A_FB[i]
+            accv = acc[:].rearrange("p (h e j) -> p h e j", h=NH, e=2)
+            for j in range(16):
+                nc.scalar.activation(
+                    out=m1[:, i, j, :, :], in_=accv[:, :, :, j], func=ACT.Copy, scale=cosf[:, t, 16 * b + j : 16 * b + j + 1]
+                )
+
+        def av_m1(t, b, acc):
+            m1 = mpool.tile([P, 32, 16], F32, name="m1v", tag="m1v", bufs=2)
+            nc.vector.tensor_tensor(
+                out=m1[:],
+                in0=acc[:].rearrange("p (x j) -> p x j", j=16),
+                in1=cosb[:, t, 16 * b : 16 * (b + 1)].unsqueeze(1).to_broadcast([P, 32, 16]),
+                op=ALU.mult,
+            )
+            return m1[:].rearrange("p (h e) j -> p h j e", e=2)
+
+        def a_m2(t, b, acc):
+            nc.vector.tensor_tensor(
+                out=ot_slice(t, b, 1).rearrange("p h (j e) -> p h j e", e=2),
+                in0=acc[:].rearrange("p (h e j) -> p h j e", h=NH, e=2)[:, :, :, ::-1],
+                in1=sgn[:, :, t, 16 * b : 16 * (b + 1)].rearrange("p e j -> p j e").unsqueeze(1).to_broadcast([P, NH, 16, 2]),
+                op=ALU.mult,
+            )
+
+        def a_add(t, b, n_b, m1r):
+            otv = ot_slice(t, b, n_b).rearrange("p h (j e) -> p h j e", e=2)
+            nc.gpsimd.tensor_tensor(out=otv, in0=m1r, in1=otv, op=ALU.add)
+
+        def b_mx(t, b):
+            pt = bank([P, 4, P], F32, "pt")
+            for hq in range(4):
+                for g in range(NG):
+                    nc.tensor.matmul_mx(
+                        out=pt[:, hq, :],
+                        lhsT=wc[:, g, 512 * b + P * hq : 512 * b + P * (hq + 1)].bitcast(FP8X4),
+                        lhsT_scale=ws[:, g, 512 * b + P * hq : 512 * b + P * (hq + 1)],
+                        rhs=xc[:, g, P * t : P * (t + 1)].bitcast(FP8X4),
+                        rhs_scale=xs[:, g, P * t : P * (t + 1)],
+                        start=(g == 0),
+                        stop=(g == NG - 1),
+                    )
+            return pt
+
+        def b_prod(t, b, pt):
+            pr = mpool.tile([P, 2, 4, P], F32, name="pr", tag="pr")
+            nc.vector.tensor_tensor(
+                out=pr[:],
+                in0=pt[:].unsqueeze(1).to_broadcast([P, 2, 4, P]),
+                in1=cst[b][:, :, P * t : P * (t + 1)].unsqueeze(2).to_broadcast([P, 2, 4, P]),
+                op=ALU.mult,
+            )
+            return pr
+
+        def b_fin(t, b, pr):
+            ob = bank([P, 4, P], F32, "ob")
+            for hq in range(4):
+                nc.tensor.matmul(out=ob[:, hq, :], lhsT=pr[:, 0, hq, :], rhs=perm_a[:], start=True, stop=False, is_transpose=True)
+                nc.tensor.matmul(out=ob[:, hq, :], lhsT=pr[:, 1, hq, :], rhs=perm_b[:], start=False, stop=True, is_transpose=True)
+            nc.scalar.copy(out=ot_slice(t, b, 1), in_=ob[:].rearrange("p q (h r) -> p (q h) r", h=4))
+
+        def store(t):
+            first, n_t = group_of[t]
+            if t == first + n_t - 1:
+                for v in range(2):
+                    nc.sync.dma_start(out=out_views[v][:, :, first : first + n_t, :], in_=ots[first][:, 8 * v : 8 * v + 8, :, :])
+
+        def kinds(t):
+            if t >= NT:
+                return ((), (), ())
+            if t % 2 == 1:
+                return (A_FB, (AV_FB,), tuple(b for b in B_FB if b != AV_FB))
+            return (A_FB, (), B_FB)
+
+        accs = {}
+        pts = {}
+        prods = {}
+        for b in kinds(0)[2]:
+            pts[(0, b)] = b_mx(0, b)
+        for b in kinds(0)[1] + kinds(0)[0]:
+            accs[(0, b)] = a_mx(0, b)
+        for t in range(NT + 1):
+            a_list, v_list, b_list = kinds(t)
+            next_b = kinds(t + 1)[2]
+            next_a = kinds(t + 1)[1] + kinds(t + 1)[0]
+            if a_list:
+                m1 = mpool.tile([P, 2, 16, NH, 2], F32, name="m1", tag="m1", bufs=3)
+                for i, b in enumerate(a_list):
+                    a_m1(t, i, accs[(t, b)], m1)
+            if t >= 1:
+                for b in kinds(t - 1)[2]:
+                    b_fin(t - 1, b, prods[b])
+                store(t - 1)
+            for i, b in enumerate(b_list):
+                prods[b] = b_prod(t, b, pts[(t, b)])
+                for nb in next_b[i : i + 1]:
+                    pts[(t + 1, nb)] = b_mx(t + 1, nb)
+            for nb in next_b[len(b_list) :]:
+                pts[(t + 1, nb)] = b_mx(t + 1, nb)
+            for na in next_a[0:1]:
+                accs[(t + 1, na)] = a_mx(t + 1, na)
+            for i, b in enumerate(v_list + a_list):
+                if b in v_list:
+                    m1v = av_m1(t, b, accs[(t, b)])
+                a_m2(t, b, accs[(t, b)])
+                if b in v_list:
+                    a_add(t, b, 1, m1v)
+                for na in next_a[i + 1 : i + 2]:
+                    accs[(t + 1, na)] = a_mx(t + 1, na)
+            if a_list:
+                a_add(t, A_FB[0], 2, m1[:].rearrange("p i j h e -> p h (i j) e"))
+            for na in next_a[len(v_list + a_list) + 1 :]:
+                accs[(t + 1, na)] = a_mx(t + 1, na)

@@ -21,12 +21,14 @@ NH = 16
 NB = 4
 NG = 2
 A_FB = (0, 1)
-B_FB = (2, 3)
-AV_FB = 3
+B3_TILES = (3, 7, 11, 15)
+B_FB = (2, 3) if B3_TILES else (2,)
 TP_TAGS = ("acc", "pt", "ob", "acc", "pt", "ob", "acc", "acc")
 TAG_BUFS = {"acc": 4, "pt": 2, "ob": 2}
+NX_HEAD = 16
 X_BEFORE_W = {3: 1, 8: 2, 13: 3}
 GROUPS = (2, 2, 2, 2, 2, 2, 1, 1, 1, 1)
+XPOS = 0
 
 
 def tile_attention_pa_kernel(tc, x_bytes, x_scale, freqs_cos, freqs_sin, wq, wk, out_0, out_1):
@@ -35,6 +37,9 @@ def tile_attention_pa_kernel(tc, x_bytes, x_scale, freqs_cos, freqs_sin, wq, wk,
         ctx.enter_context(tc.manual_schedule())
         const = ctx.enter_context(tc.tile_pool(name="const", bufs=1))
         psum = ctx.enter_context(tc.psum_pool(name="psum", bufs=2))
+        head = ExitStack()
+        xin = head.enter_context(tc.tile_pool(name="xin", bufs=1))
+        xwork = head.enter_context(tc.tile_pool(name="xwork", bufs=4))
         counters = {"tp": 0}
 
         def bank(shape, dtype, tag):
@@ -55,7 +60,7 @@ def tile_attention_pa_kernel(tc, x_bytes, x_scale, freqs_cos, freqs_sin, wq, wk,
         sel_c = {}
         sel_s = {}
         for b in B_FB:
-            cst[b] = const.tile([P, 2, NT * P], BF16, name="cst%d" % b)
+            cst[b] = const.tile([P, 2, (NT if b == 2 else len(B3_TILES)) * P], BF16, name="cst%d" % b)
             sel_c[b] = const.tile([P, P], BF16, name="selc%d" % b)
             sel_s[b] = const.tile([P, P], BF16, name="sels%d" % b)
         wc = const.tile([P, NG, NB * 512], U32, name="wc", align_bytes=64)
@@ -67,20 +72,44 @@ def tile_attention_pa_kernel(tc, x_bytes, x_scale, freqs_cos, freqs_sin, wq, wk,
         perm_w = const.tile([P, P], F32, name="perm_w")
         perm_a = const.tile([P, P], F32, name="perm_a")
         perm_b = const.tile([P, P], F32, name="perm_b")
+        xbytes = [xin.tile([P, 4, D], U8, name="xbytes%d" % c) for c in range(4)]
+        x_view = x_bytes.rearrange("o (p t) k -> (o p) t k", t=NT)
+        cos_view = freqs_cos.rearrange("(p t) j -> p t j", t=NT)
+        sin_view = freqs_sin.rearrange("(p t) j -> p t j", t=NT)
+        xbf = {}
+        xg = {}
 
-        with ExitStack() as head:
-            xin = head.enter_context(tc.tile_pool(name="xin", bufs=1))
-            xwork = head.enter_context(tc.tile_pool(name="xwork", bufs=4))
+        def transposes(words, permutation, tag):
+            tp = bank([P, 4, P], F32, tag) if tag else tp_bank([P, 4, P], F32)
+            for g in range(NG):
+                for u in range(2):
+                    nc.tensor.transpose(tp[:, 2 * g + u, :], words[:, 256 * g + u : 256 * (g + 1) : 2], permutation[:])
+            return tp
+
+        def x_prod(t):
+            xb = xwork.tile([P, D], BF16, name="xbf", tag="xbf", bufs=16)
+            nc.vector.tensor_tensor(out=xb[:], in0=xbytes[t // 4][:, t % 4, :].bitcast(FP8), in1=scale_bc[:], op=ALU.mult)
+            xbf[t] = xb
+
+        def x_tr(t, tag):
+            if t % 4 == 0:
+                xg[t // 4] = xwork.tile([P, NG, 4, P, 2], F32, name="xg", tag="xg", align_bytes=64)
+            tp = transposes(xbf[t][:].bitcast(F32), ident, tag)
+            nc.scalar.copy(out=xg[t // 4][:, :, t % 4, :, :], in_=tp[:].rearrange("p (g u) n -> p g n u", u=2))
+
+        def x_quant(c):
+            for g in range(NG):
+                nc.vector.quantize_mx(
+                    out=xc[:, g, 512 * c : 512 * (c + 1)].bitcast(FP8X4),
+                    scales=xs[:, g, 512 * c : 512 * (c + 1)],
+                    in_=xg[c][:, g, :, :, :].rearrange("p a n u -> p (a n u)").bitcast(BF16),
+                )
+
+        with head:
             wraw_pool = head.enter_context(tc.tile_pool(name="wraw", bufs=NH))
             wgp = head.enter_context(tc.tile_pool(name="wgp", bufs=1))
-            xbytes = [xin.tile([P, 4, D], U8, name="xbytes%d" % c) for c in range(4)]
             wg = [wgp.tile([P, NB, NH, 32, 2], F32, name="wg%d" % g, align_bytes=64) for g in range(NG)]
-            x_view = x_bytes.rearrange("o (p t) k -> (o p) t k", t=NT)
-            cos_view = freqs_cos.rearrange("(p t) j -> p t j", t=NT)
-            sin_view = freqs_sin.rearrange("(p t) j -> p t j", t=NT)
             wraw = []
-            xbf = []
-            xg = []
 
             nc.sync.dma_start(out=xbytes[0][:, 0:1, :], in_=x_view[:, 0:1, :])
             nc.sync.dma_start(out=scale_bc[:], in_=x_scale.rearrange("a b k -> (a b k)").partition_broadcast(P))
@@ -122,36 +151,17 @@ def tile_attention_pa_kernel(tc, x_bytes, x_scale, freqs_cos, freqs_sin, wq, wk,
                 nc.vector.tensor_copy(out=sv[:, :, 0, :], in_=src)
                 nc.vector.tensor_scalar(out=sv[:, :, 1, :], in0=src, scalar1=-1.0, scalar2=None, op0=ALU.mult)
 
-            def transposes(words, permutation):
-                tp = tp_bank([P, 4, P], F32)
-                for g in range(NG):
-                    for u in range(2):
-                        nc.tensor.transpose(tp[:, 2 * g + u, :], words[:, 256 * g + u : 256 * (g + 1) : 2], permutation[:])
-                return tp
-
-            def x_quant(c):
-                for g in range(NG):
-                    nc.vector.quantize_mx(
-                        out=xc[:, g, 512 * c : 512 * (c + 1)].bitcast(FP8X4),
-                        scales=xs[:, g, 512 * c : 512 * (c + 1)],
-                        in_=xg[c][:, g, :, :, :].rearrange("p a n u -> p (a n u)").bitcast(BF16),
-                    )
-
+            for t in range(NX_HEAD):
+                x_prod(t)
             for t in range(NT):
-                xb = xwork.tile([P, D], BF16, name="xbf", tag="xbf", bufs=NT)
-                nc.vector.tensor_tensor(out=xb[:], in0=xbytes[t // 4][:, t % 4, :].bitcast(FP8), in1=scale_bc[:], op=ALU.mult)
-                xbf.append(xb)
-            for t in range(NT):
-                if t % 4 == 0:
-                    xg.append(xwork.tile([P, NG, 4, P, 2], F32, name="xg", tag="xg", align_bytes=64))
-                tp = transposes(xbf[t][:].bitcast(F32), ident)
-                nc.scalar.copy(out=xg[t // 4][:, :, t % 4, :, :], in_=tp[:].rearrange("p (g u) n -> p g n u", u=2))
-                tp = transposes(wraw[t][:].bitcast(F32), perm_w)
+                if t < NX_HEAD:
+                    x_tr(t, None)
+                tp = transposes(wraw[t][:].bitcast(F32), perm_w, None)
                 for g in range(NG):
                     nc.scalar.copy(
                         out=wg[g][:, :, t, :, :], in_=tp[:, 2 * g : 2 * g + 2, :].rearrange("p u (b r) -> p b r u", b=NB)
                     )
-                if t in (3, 7, 11):
+                if t < NX_HEAD and t % 4 == 3:
                     x_quant(t // 4)
             for c in range(4):
                 tpb = bank([P, 4, P], BF16, "ob")
@@ -159,19 +169,22 @@ def tile_attention_pa_kernel(tc, x_bytes, x_scale, freqs_cos, freqs_sin, wq, wk,
                     nc.tensor.transpose(tpb[:, i, :], tab2[:, 4 * c + i, :], identb[:])
                 nc.scalar.copy(out=tabT[:, 512 * c : 512 * (c + 1)], in_=tpb[:].rearrange("p i n -> p (i n)"))
             for c in range(4):
-                for b in B_FB:
-                    pm = bank([P, 2, 512], BF16, "ob")
-                    for v, sel in enumerate((sel_c[b], sel_s[b])):
-                        nc.tensor.matmul(out=pm[:, v, :], lhsT=sel[:], rhs=tabT[:, 512 * c : 512 * (c + 1)], start=True, stop=True)
-                    nc.scalar.copy(out=cst[b][:, :, 512 * c : 512 * (c + 1)], in_=pm[:])
-            for b in B_FB + A_FB:
+                pm = bank([P, 2, 512], BF16, "ob")
+                for v, sel in enumerate((sel_c[2], sel_s[2])):
+                    nc.tensor.matmul(out=pm[:, v, :], lhsT=sel[:], rhs=tabT[:, 512 * c : 512 * (c + 1)], start=True, stop=True)
+                nc.scalar.copy(out=cst[2][:, :, 512 * c : 512 * (c + 1)], in_=pm[:])
+            for i, t in enumerate(B3_TILES):
+                pm = bank([P, 2, P], BF16, "ob")
+                for v, sel in enumerate((sel_c[3], sel_s[3])):
+                    nc.tensor.matmul(out=pm[:, v, :], lhsT=sel[:], rhs=tabT[:, P * t : P * (t + 1)], start=True, stop=True)
+                nc.scalar.copy(out=cst[3][:, :, P * i : P * (i + 1)], in_=pm[:])
+            for b in (2, 3, 0, 1):
                 for g in range(NG):
                     nc.vector.quantize_mx(
                         out=wc[:, g, 512 * b : 512 * (b + 1)].bitcast(FP8X4),
                         scales=ws[:, g, 512 * b : 512 * (b + 1)],
                         in_=wg[g][:, b, :, :, :].rearrange("p h r u -> p (h r u)").bitcast(BF16),
                     )
-            x_quant(3)
             nc.scalar.copy(out=cosf[:], in_=cosb[:, :, 0:32])
             nc.scalar.activation(out=sgn[:, 0, :, :], in_=sgn[:, 1, :, :], func=ACT.Copy, scale=-1.0)
 
@@ -254,12 +267,15 @@ def tile_attention_pa_kernel(tc, x_bytes, x_scale, freqs_cos, freqs_sin, wq, wk,
                     )
             return pt
 
+        def tab_col(t, b):
+            return t if b == 2 else B3_TILES.index(t)
+
         def b_prod(t, b, pt):
             pr = mpool.tile([P, 2, 4, P], F32, name="pr", tag="pr")
             nc.vector.tensor_tensor(
                 out=pr[:],
                 in0=pt[:].unsqueeze(1).to_broadcast([P, 2, 4, P]),
-                in1=cst[b][:, :, P * t : P * (t + 1)].unsqueeze(2).to_broadcast([P, 2, 4, P]),
+                in1=cst[b][:, :, P * tab_col(t, b) : P * (tab_col(t, b) + 1)].unsqueeze(2).to_broadcast([P, 2, 4, P]),
                 op=ALU.mult,
             )
             return pr
@@ -280,9 +296,9 @@ def tile_attention_pa_kernel(tc, x_bytes, x_scale, freqs_cos, freqs_sin, wq, wk,
         def kinds(t):
             if t >= NT:
                 return ((), (), ())
-            if t % 2 == 1:
-                return (A_FB, (AV_FB,), tuple(b for b in B_FB if b != AV_FB))
-            return (A_FB, (), B_FB)
+            if t in B3_TILES:
+                return (A_FB, (), (2, 3))
+            return (A_FB, (3,), (2,))
 
         accs = {}
         pts = {}
@@ -295,20 +311,29 @@ def tile_attention_pa_kernel(tc, x_bytes, x_scale, freqs_cos, freqs_sin, wq, wk,
             a_list, v_list, b_list = kinds(t)
             next_b = kinds(t + 1)[2]
             next_a = kinds(t + 1)[1] + kinds(t + 1)[0]
+            xp = NX_HEAD + t
             if a_list:
                 m1 = mpool.tile([P, 2, 16, NH, 2], F32, name="m1", tag="m1", bufs=3)
                 for i, b in enumerate(a_list):
                     a_m1(t, i, accs[(t, b)], m1)
+            if XPOS == 0 and xp < NT:
+                x_prod(xp)
             if t >= 1:
                 for b in kinds(t - 1)[2]:
                     b_fin(t - 1, b, prods[b])
                 store(t - 1)
+            if NX_HEAD <= xp - 1 < NT:
+                x_tr(xp - 1, "ob")
+            if NX_HEAD <= xp - 2 < NT and (xp - 2) % 4 == 3:
+                x_quant((xp - 2) // 4)
             for i, b in enumerate(b_list):
                 prods[b] = b_prod(t, b, pts[(t, b)])
                 for nb in next_b[i : i + 1]:
                     pts[(t + 1, nb)] = b_mx(t + 1, nb)
             for nb in next_b[len(b_list) :]:
                 pts[(t + 1, nb)] = b_mx(t + 1, nb)
+            if XPOS == 1 and xp < NT:
+                x_prod(xp)
             for na in next_a[0:1]:
                 accs[(t + 1, na)] = a_mx(t + 1, na)
             for i, b in enumerate(v_list + a_list):
@@ -319,7 +344,11 @@ def tile_attention_pa_kernel(tc, x_bytes, x_scale, freqs_cos, freqs_sin, wq, wk,
                     a_add(t, b, 1, m1v)
                 for na in next_a[i + 1 : i + 2]:
                     accs[(t + 1, na)] = a_mx(t + 1, na)
+            if XPOS == 2 and xp < NT:
+                x_prod(xp)
             if a_list:
                 a_add(t, A_FB[0], 2, m1[:].rearrange("p i j h e -> p h (i j) e"))
+            if XPOS == 3 and xp < NT:
+                x_prod(xp)
             for na in next_a[len(v_list + a_list) + 1 :]:
                 accs[(t + 1, na)] = a_mx(t + 1, na)

@@ -22,13 +22,18 @@ NB = 4
 NG = 2
 A_FB = (0, 1)
 B3_TILES = (3, 7, 11, 15)
-B_FB = (2, 3) if B3_TILES else (2,)
+FLEX = 2
+FIXB = 3
+B_FB = (FIXB, FLEX) if B3_TILES else (FIXB,)
 TP_TAGS = ("acc", "pt", "ob", "acc", "pt", "ob", "acc", "acc")
 TAG_BUFS = {"acc": 4, "pt": 2, "ob": 2}
 NX_HEAD = 16
 X_BEFORE_W = {3: 1, 8: 2, 13: 3}
 GROUPS = (2, 2, 2, 2, 2, 2, 1, 1, 1, 1)
 XPOS = 0
+VADD_FROM = 14
+LOADS = (("x0", 0), ("s", 0), ("x0r", 0), ("w", 0), ("w", 1), ("w", 2), ("x", 1), ("w", 3), ("w", 4), ("w", 5), ("w", 6), ("w", 7), ("x", 2), ("w", 8), ("w", 9), ("w", 10), ("w", 11), ("w", 12), ("x", 3), ("w", 13), ("w", 14), ("w", 15))
+HEAD_ORDER = (("x", 0), ("w", 0), ("x", 1), ("w", 1), ("x", 2), ("w", 2), ("x", 3), ("w", 3), ("x", 4), ("w", 4), ("x", 5), ("w", 5), ("x", 6), ("w", 6), ("x", 7), ("w", 7), ("x", 8), ("w", 8), ("x", 9), ("w", 9), ("x", 10), ("w", 10), ("x", 11), ("w", 11), ("x", 12), ("w", 12), ("x", 13), ("w", 13), ("x", 14), ("w", 14), ("x", 15), ("w", 15))
 
 
 def tile_attention_pa_kernel(tc, x_bytes, x_scale, freqs_cos, freqs_sin, wq, wk, out_0, out_1):
@@ -60,7 +65,7 @@ def tile_attention_pa_kernel(tc, x_bytes, x_scale, freqs_cos, freqs_sin, wq, wk,
         sel_c = {}
         sel_s = {}
         for b in B_FB:
-            cst[b] = const.tile([P, 2, (NT if b == 2 else len(B3_TILES)) * P], BF16, name="cst%d" % b)
+            cst[b] = const.tile([P, 2, (NT if b == FIXB else len(B3_TILES)) * P], BF16, name="cst%d" % b)
             sel_c[b] = const.tile([P, P], BF16, name="selc%d" % b)
             sel_s[b] = const.tile([P, P], BF16, name="sels%d" % b)
         wc = const.tile([P, NG, NB * 512], U32, name="wc", align_bytes=64)
@@ -111,17 +116,20 @@ def tile_attention_pa_kernel(tc, x_bytes, x_scale, freqs_cos, freqs_sin, wq, wk,
             wg = [wgp.tile([P, NB, NH, 32, 2], F32, name="wg%d" % g, align_bytes=64) for g in range(NG)]
             wraw = []
 
-            nc.sync.dma_start(out=xbytes[0][:, 0:1, :], in_=x_view[:, 0:1, :])
-            nc.sync.dma_start(out=scale_bc[:], in_=x_scale.rearrange("a b k -> (a b k)").partition_broadcast(P))
-            nc.sync.dma_start(out=xbytes[0][:, 1:4, :], in_=x_view[:, 1:4, :])
             for h in range(NH):
-                if h in X_BEFORE_W:
-                    c = X_BEFORE_W[h]
-                    nc.sync.dma_start(out=xbytes[c][:], in_=x_view[:, 4 * c : 4 * c + 4, :])
-                w = wq if h < 8 else wk
-                wr = wraw_pool.tile([P, D], BF16, name="wr", tag="wr")
-                nc.sync.dma_start(out=wr[:], in_=w[(h % 8) * P : (h % 8 + 1) * P, :])
-                wraw.append(wr)
+                wraw.append(wraw_pool.tile([P, D], BF16, name="wr", tag="wr"))
+            for kind, i in LOADS:
+                if kind == "w":
+                    w = wq if i < 8 else wk
+                    nc.sync.dma_start(out=wraw[i][:], in_=w[(i % 8) * P : (i % 8 + 1) * P, :])
+                elif kind == "x0":
+                    nc.sync.dma_start(out=xbytes[0][:, 0:1, :], in_=x_view[:, 0:1, :])
+                elif kind == "x0r":
+                    nc.sync.dma_start(out=xbytes[0][:, 1:4, :], in_=x_view[:, 1:4, :])
+                elif kind == "x":
+                    nc.sync.dma_start(out=xbytes[i][:], in_=x_view[:, 4 * i : 4 * i + 4, :])
+                elif kind == "s":
+                    nc.sync.dma_start(out=scale_bc[:], in_=x_scale.rearrange("a b k -> (a b k)").partition_broadcast(P))
             nc.sync.dma_start(out=tab2[:, :, 0:64], in_=sin_view)
             nc.sync.dma_start(out=tab2[:, :, 64:128], in_=cos_view)
             nc.sync.dma_start(out=cosb[:], in_=cos_view)
@@ -153,16 +161,17 @@ def tile_attention_pa_kernel(tc, x_bytes, x_scale, freqs_cos, freqs_sin, wq, wk,
 
             for t in range(NX_HEAD):
                 x_prod(t)
-            for t in range(NT):
-                if t < NX_HEAD:
+            for kind, t in HEAD_ORDER:
+                if kind == "x":
                     x_tr(t, None)
-                tp = transposes(wraw[t][:].bitcast(F32), perm_w, None)
-                for g in range(NG):
-                    nc.scalar.copy(
-                        out=wg[g][:, :, t, :, :], in_=tp[:, 2 * g : 2 * g + 2, :].rearrange("p u (b r) -> p b r u", b=NB)
-                    )
-                if t < NX_HEAD and t % 4 == 3:
-                    x_quant(t // 4)
+                    if t % 4 == 3 and t < 12:
+                        x_quant(t // 4)
+                else:
+                    tp = transposes(wraw[t][:].bitcast(F32), perm_w, None)
+                    for g in range(NG):
+                        nc.scalar.copy(
+                            out=wg[g][:, :, t, :, :], in_=tp[:, 2 * g : 2 * g + 2, :].rearrange("p u (b r) -> p b r u", b=NB)
+                        )
             for c in range(4):
                 tpb = bank([P, 4, P], BF16, "ob")
                 for i in range(4):
@@ -170,21 +179,22 @@ def tile_attention_pa_kernel(tc, x_bytes, x_scale, freqs_cos, freqs_sin, wq, wk,
                 nc.scalar.copy(out=tabT[:, 512 * c : 512 * (c + 1)], in_=tpb[:].rearrange("p i n -> p (i n)"))
             for c in range(4):
                 pm = bank([P, 2, 512], BF16, "ob")
-                for v, sel in enumerate((sel_c[2], sel_s[2])):
+                for v, sel in enumerate((sel_c[FIXB], sel_s[FIXB])):
                     nc.tensor.matmul(out=pm[:, v, :], lhsT=sel[:], rhs=tabT[:, 512 * c : 512 * (c + 1)], start=True, stop=True)
-                nc.scalar.copy(out=cst[2][:, :, 512 * c : 512 * (c + 1)], in_=pm[:])
+                nc.scalar.copy(out=cst[FIXB][:, :, 512 * c : 512 * (c + 1)], in_=pm[:])
             for i, t in enumerate(B3_TILES):
                 pm = bank([P, 2, P], BF16, "ob")
-                for v, sel in enumerate((sel_c[3], sel_s[3])):
+                for v, sel in enumerate((sel_c[FLEX], sel_s[FLEX])):
                     nc.tensor.matmul(out=pm[:, v, :], lhsT=sel[:], rhs=tabT[:, P * t : P * (t + 1)], start=True, stop=True)
-                nc.scalar.copy(out=cst[3][:, :, P * i : P * (i + 1)], in_=pm[:])
-            for b in (2, 3, 0, 1):
+                nc.scalar.copy(out=cst[FLEX][:, :, P * i : P * (i + 1)], in_=pm[:])
+            for b in (3, 2, 0, 1):
                 for g in range(NG):
                     nc.vector.quantize_mx(
                         out=wc[:, g, 512 * b : 512 * (b + 1)].bitcast(FP8X4),
                         scales=ws[:, g, 512 * b : 512 * (b + 1)],
                         in_=wg[g][:, b, :, :, :].rearrange("p h r u -> p (h r u)").bitcast(BF16),
                     )
+            x_quant(3)
             nc.scalar.copy(out=cosf[:], in_=cosb[:, :, 0:32])
             nc.scalar.activation(out=sgn[:, 0, :, :], in_=sgn[:, 1, :, :], func=ACT.Copy, scale=-1.0)
 
@@ -230,15 +240,13 @@ def tile_attention_pa_kernel(tc, x_bytes, x_scale, freqs_cos, freqs_sin, wq, wk,
                     out=m1[:, i, j, :, :], in_=accv[:, :, :, j], func=ACT.Copy, scale=cosf[:, t, 16 * b + j : 16 * b + j + 1]
                 )
 
-        def av_m1(t, b, acc):
-            m1 = mpool.tile([P, 32, 16], F32, name="m1v", tag="m1v", bufs=2)
+        def av_m1(t, b, acc, m1):
             nc.vector.tensor_tensor(
-                out=m1[:],
-                in0=acc[:].rearrange("p (x j) -> p x j", j=16),
-                in1=cosb[:, t, 16 * b : 16 * (b + 1)].unsqueeze(1).to_broadcast([P, 32, 16]),
+                out=m1[:, 2, :, :, :].rearrange("p j h e -> p j (h e)"),
+                in0=acc[:].rearrange("p (x j) -> p j x", j=16),
+                in1=cosb[:, t, 16 * b : 16 * (b + 1)].unsqueeze(2).to_broadcast([P, 16, 32]),
                 op=ALU.mult,
             )
-            return m1[:].rearrange("p (h e) j -> p h j e", e=2)
 
         def a_m2(t, b, acc):
             nc.vector.tensor_tensor(
@@ -268,7 +276,7 @@ def tile_attention_pa_kernel(tc, x_bytes, x_scale, freqs_cos, freqs_sin, wq, wk,
             return pt
 
         def tab_col(t, b):
-            return t if b == 2 else B3_TILES.index(t)
+            return t if b == FIXB else B3_TILES.index(t)
 
         def b_prod(t, b, pt):
             pr = mpool.tile([P, 2, 4, P], F32, name="pr", tag="pr")
@@ -287,19 +295,32 @@ def tile_attention_pa_kernel(tc, x_bytes, x_scale, freqs_cos, freqs_sin, wq, wk,
                 nc.tensor.matmul(out=ob[:, hq, :], lhsT=pr[:, 1, hq, :], rhs=perm_b[:], start=False, stop=True, is_transpose=True)
             nc.scalar.copy(out=ot_slice(t, b, 1), in_=ob[:].rearrange("p q (h r) -> p (q h) r", h=4))
 
+        def store_half(t, v):
+            first, n_t = group_of[t]
+            nc.sync.dma_start(out=out_views[v][:, :, first : first + n_t, :], in_=ots[first][:, 8 * v : 8 * v + 8, :, :])
+
         def store(t):
             first, n_t = group_of[t]
             if t == first + n_t - 1:
                 for v in range(2):
-                    nc.sync.dma_start(out=out_views[v][:, :, first : first + n_t, :], in_=ots[first][:, 8 * v : 8 * v + 8, :, :])
+                    store_half(t, v)
+
+        def last_adds(t, n_b, m1r):
+            otv = ot_slice(t, A_FB[0], n_b).rearrange("p h (j e) -> p h j e", e=2)
+            for v in range(2):
+                nc.vector.tensor_tensor(
+                    out=otv[:, 8 * v : 8 * v + 8, :, :], in0=m1r[:, 8 * v : 8 * v + 8, :, :], in1=otv[:, 8 * v : 8 * v + 8, :, :], op=ALU.add
+                )
+                store_half(t, v)
 
         def kinds(t):
             if t >= NT:
                 return ((), (), ())
             if t in B3_TILES:
-                return (A_FB, (), (2, 3))
-            return (A_FB, (3,), (2,))
+                return (A_FB, (), (FIXB, FLEX))
+            return (A_FB, (FLEX,), (FIXB,))
 
+        late = {}
         accs = {}
         pts = {}
         prods = {}
@@ -307,21 +328,27 @@ def tile_attention_pa_kernel(tc, x_bytes, x_scale, freqs_cos, freqs_sin, wq, wk,
             pts[(0, b)] = b_mx(0, b)
         for b in kinds(0)[1] + kinds(0)[0]:
             accs[(0, b)] = a_mx(0, b)
-        for t in range(NT + 1):
+        for t in range(NT):
             a_list, v_list, b_list = kinds(t)
             next_b = kinds(t + 1)[2]
             next_a = kinds(t + 1)[1] + kinds(t + 1)[0]
             xp = NX_HEAD + t
+            early_fin = t >= 99
+            if early_fin:
+                for b in kinds(t - 1)[2]:
+                    b_fin(t - 1, b, prods[b])
+                store(t - 1)
             if a_list:
-                m1 = mpool.tile([P, 2, 16, NH, 2], F32, name="m1", tag="m1", bufs=3)
+                m1 = mpool.tile([P, 3, 16, NH, 2], F32, name="m1", tag="m1", bufs=3)
                 for i, b in enumerate(a_list):
                     a_m1(t, i, accs[(t, b)], m1)
             if XPOS == 0 and xp < NT:
                 x_prod(xp)
-            if t >= 1:
+            if t >= 1 and not early_fin:
                 for b in kinds(t - 1)[2]:
                     b_fin(t - 1, b, prods[b])
-                store(t - 1)
+                if t - 1 < VADD_FROM:
+                    store(t - 1)
             if NX_HEAD <= xp - 1 < NT:
                 x_tr(xp - 1, "ob")
             if NX_HEAD <= xp - 2 < NT and (xp - 2) % 4 == 3:
@@ -332,22 +359,29 @@ def tile_attention_pa_kernel(tc, x_bytes, x_scale, freqs_cos, freqs_sin, wq, wk,
                     pts[(t + 1, nb)] = b_mx(t + 1, nb)
             for nb in next_b[len(b_list) :]:
                 pts[(t + 1, nb)] = b_mx(t + 1, nb)
+            if t == NT - 1:
+                for b in b_list:
+                    b_fin(t, b, prods[b])
             if XPOS == 1 and xp < NT:
                 x_prod(xp)
             for na in next_a[0:1]:
                 accs[(t + 1, na)] = a_mx(t + 1, na)
             for i, b in enumerate(v_list + a_list):
                 if b in v_list:
-                    m1v = av_m1(t, b, accs[(t, b)])
+                    av_m1(t, b, accs[(t, b)], m1)
                 a_m2(t, b, accs[(t, b)])
-                if b in v_list:
-                    a_add(t, b, 1, m1v)
                 for na in next_a[i + 1 : i + 2]:
                     accs[(t + 1, na)] = a_mx(t + 1, na)
             if XPOS == 2 and xp < NT:
                 x_prod(xp)
-            if a_list:
-                a_add(t, A_FB[0], 2, m1[:].rearrange("p i j h e -> p h (i j) e"))
+            n_b = 2 + len(v_list)
+            if t >= VADD_FROM:
+                late[t] = (n_b, m1[:, 0:n_b, :, :, :].rearrange("p i j h e -> p h (i j) e"))
+            else:
+                a_add(t, A_FB[0], n_b, m1[:, 0:n_b, :, :, :].rearrange("p i j h e -> p h (i j) e"))
+            if t == NT - 1:
+                for tl in range(VADD_FROM, NT):
+                    last_adds(tl, late[tl][0], late[tl][1])
             if XPOS == 3 and xp < NT:
                 x_prod(xp)
             for na in next_a[len(v_list + a_list) + 1 :]:

@@ -31,9 +31,16 @@ NX_HEAD = 16
 X_BEFORE_W = {3: 1, 8: 2, 13: 3}
 GROUPS = (2, 2, 2, 2, 2, 2, 1, 1, 1, 1)
 XPOS = 0
+TAB_OB = True
+PE_SCALE = True
+NCHUNK = 2
+LATE_EARLY = False
+JV_LAST = 0
+XQ_INLINE = (0, 1, 2)
+JV = 0
 VADD_FROM = 14
-LOADS = (("x0", 0), ("s", 0), ("x0r", 0), ("w", 0), ("w", 1), ("w", 2), ("x", 1), ("w", 3), ("w", 4), ("w", 5), ("w", 6), ("w", 7), ("x", 2), ("w", 8), ("w", 9), ("w", 10), ("w", 11), ("w", 12), ("x", 3), ("w", 13), ("w", 14), ("w", 15))
-HEAD_ORDER = (("x", 0), ("w", 0), ("x", 1), ("w", 1), ("x", 2), ("w", 2), ("x", 3), ("w", 3), ("x", 4), ("w", 4), ("x", 5), ("w", 5), ("x", 6), ("w", 6), ("x", 7), ("w", 7), ("x", 8), ("w", 8), ("x", 9), ("w", 9), ("x", 10), ("w", 10), ("x", 11), ("w", 11), ("x", 12), ("w", 12), ("x", 13), ("w", 13), ("x", 14), ("w", 14), ("x", 15), ("w", 15))
+LOADS = (("s8", 0), ("x0", 0), ("w", 0), ("w", 1), ("x0r", 0), ("w", 2), ("w", 3), ("x", 1), ("w", 4), ("w", 5), ("w", 6), ("w", 7), ("w", 8), ("x", 2), ("w", 9), ("w", 10), ("w", 11), ("w", 12), ("x", 3), ("w", 13), ("w", 14), ("w", 15))
+HEAD_ORDER = (("w", 0), ("w", 1), ("x", 0), ("w", 2), ("x", 1), ("w", 3), ("x", 2), ("w", 4), ("x", 3), ("w", 5), ("x", 4), ("w", 6), ("x", 5), ("w", 7), ("x", 6), ("w", 8), ("x", 7), ("w", 9), ("x", 8), ("w", 10), ("x", 9), ("w", 11), ("x", 10), ("w", 12), ("x", 11), ("w", 13), ("x", 12), ("w", 14), ("x", 13), ("w", 15), ("x", 14), ("x", 15), ("tt", 0), ("tt", 1), ("tt", 2), ("tt", 3), ("ts", 0), ("ts", 1), ("ts", 2), ("ts", 3), ("tf", 0), ("tf", 1), ("tf", 2), ("tf", 3), ("cs", 0))
 
 
 def tile_attention_pa_kernel(tc, x_bytes, x_scale, freqs_cos, freqs_sin, wq, wk, out_0, out_1):
@@ -54,6 +61,9 @@ def tile_attention_pa_kernel(tc, x_bytes, x_scale, freqs_cos, freqs_sin, wq, wk,
             tag = TP_TAGS[counters["tp"] % 8]
             counters["tp"] += 1
             return bank(shape, dtype, tag)
+
+        def tab_bank(shape, dtype):
+            return bank(shape, dtype, "ob") if TAB_OB else tp_bank(shape, dtype)
 
         scale_bc = const.tile([P, D], F32, name="scale_bc")
         cosb = const.tile([P, NT, 64], BF16, name="cosb")
@@ -93,7 +103,15 @@ def tile_attention_pa_kernel(tc, x_bytes, x_scale, freqs_cos, freqs_sin, wq, wk,
 
         def x_prod(t):
             xb = xwork.tile([P, D], BF16, name="xbf", tag="xbf", bufs=16)
-            nc.vector.tensor_tensor(out=xb[:], in0=xbytes[t // 4][:, t % 4, :].bitcast(FP8), in1=scale_bc[:], op=ALU.mult)
+            n_c = NCHUNK if t == 0 else 1
+            w_c = D // n_c
+            for c in range(n_c):
+                nc.vector.tensor_tensor(
+                    out=xb[:, w_c * c : w_c * (c + 1)],
+                    in0=xbytes[t // 4][:, t % 4, w_c * c : w_c * (c + 1)].bitcast(FP8),
+                    in1=scale_bc[:, w_c * c : w_c * (c + 1)],
+                    op=ALU.mult,
+                )
             xbf[t] = xb
 
         def x_tr(t, tag):
@@ -116,6 +134,10 @@ def tile_attention_pa_kernel(tc, x_bytes, x_scale, freqs_cos, freqs_sin, wq, wk,
             wg = [wgp.tile([P, NB, NH, 32, 2], F32, name="wg%d" % g, align_bytes=64) for g in range(NG)]
             wraw = []
 
+            s8 = wgp.tile([P, P], F32, name="s8")
+            sp = wgp.tile([P, 8], F32, name="sp")
+            if PE_SCALE:
+                nc.vector.memset(s8[:], 0.0)
             for h in range(NH):
                 wraw.append(wraw_pool.tile([P, D], BF16, name="wr", tag="wr"))
             for kind, i in LOADS:
@@ -128,6 +150,13 @@ def tile_attention_pa_kernel(tc, x_bytes, x_scale, freqs_cos, freqs_sin, wq, wk,
                     nc.sync.dma_start(out=xbytes[0][:, 1:4, :], in_=x_view[:, 1:4, :])
                 elif kind == "x":
                     nc.sync.dma_start(out=xbytes[i][:], in_=x_view[:, 4 * i : 4 * i + 4, :])
+                elif kind == "sc":
+                    nc.sync.dma_start(
+                        out=scale_bc[:, 256 * i : 256 * (i + 1)],
+                        in_=x_scale.rearrange("a b k -> (a b k)")[256 * i : 256 * (i + 1)].partition_broadcast(P),
+                    )
+                elif kind == "s8":
+                    nc.sync.dma_start(out=s8[0:8, :], in_=x_scale.rearrange("a b (c n) -> (a b c) n", n=P))
                 elif kind == "s":
                     nc.sync.dma_start(out=scale_bc[:], in_=x_scale.rearrange("a b k -> (a b k)").partition_broadcast(P))
             nc.sync.dma_start(out=tab2[:, :, 0:64], in_=sin_view)
@@ -159,34 +188,46 @@ def tile_attention_pa_kernel(tc, x_bytes, x_scale, freqs_cos, freqs_sin, wq, wk,
                 nc.vector.tensor_copy(out=sv[:, :, 0, :], in_=src)
                 nc.vector.tensor_scalar(out=sv[:, :, 1, :], in0=src, scalar1=-1.0, scalar2=None, op0=ALU.mult)
 
+            if PE_SCALE:
+                tp0 = tp_bank([P, P], F32)
+                nc.tensor.transpose(tp0[:], s8[:], ident[:])
+                nc.scalar.copy(out=sp[:], in_=tp0[:, 0:8])
+                for half in range(2):
+                    tpb = tp_bank([P, 4, P], F32)
+                    for i in range(4):
+                        nc.tensor.transpose(tpb[:, i, :], sp[:, 4 * half + i : 4 * half + i + 1].to_broadcast([P, P]), ident[:])
+                    nc.scalar.copy(out=scale_bc[:, 512 * half : 512 * (half + 1)], in_=tpb[:].rearrange("p i n -> p (i n)"))
             for t in range(NX_HEAD):
                 x_prod(t)
             for kind, t in HEAD_ORDER:
                 if kind == "x":
                     x_tr(t, None)
-                    if t % 4 == 3 and t < 12:
+                    if t % 4 == 3 and t // 4 in XQ_INLINE:
                         x_quant(t // 4)
+                elif kind == "cs":
+                    nc.scalar.copy(out=cosf[:], in_=cosb[:, :, 0:32])
+                    nc.scalar.activation(out=sgn[:, 0, :, :], in_=sgn[:, 1, :, :], func=ACT.Copy, scale=-1.0)
+                elif kind == "tt":
+                    tpb = tab_bank([P, 4, P], BF16)
+                    for i in range(4):
+                        nc.tensor.transpose(tpb[:, i, :], tab2[:, 4 * t + i, :], identb[:])
+                    nc.scalar.copy(out=tabT[:, 512 * t : 512 * (t + 1)], in_=tpb[:].rearrange("p i n -> p (i n)"))
+                elif kind == "ts":
+                    pm = tab_bank([P, 2, 512], BF16)
+                    for v, sel in enumerate((sel_c[FIXB], sel_s[FIXB])):
+                        nc.tensor.matmul(out=pm[:, v, :], lhsT=sel[:], rhs=tabT[:, 512 * t : 512 * (t + 1)], start=True, stop=True)
+                    nc.scalar.copy(out=cst[FIXB][:, :, 512 * t : 512 * (t + 1)], in_=pm[:])
+                elif kind == "tf":
+                    pm = tab_bank([P, 2, P], BF16)
+                    for v, sel in enumerate((sel_c[FLEX], sel_s[FLEX])):
+                        nc.tensor.matmul(out=pm[:, v, :], lhsT=sel[:], rhs=tabT[:, P * B3_TILES[t] : P * (B3_TILES[t] + 1)], start=True, stop=True)
+                    nc.scalar.copy(out=cst[FLEX][:, :, P * t : P * (t + 1)], in_=pm[:])
                 else:
                     tp = transposes(wraw[t][:].bitcast(F32), perm_w, None)
                     for g in range(NG):
                         nc.scalar.copy(
                             out=wg[g][:, :, t, :, :], in_=tp[:, 2 * g : 2 * g + 2, :].rearrange("p u (b r) -> p b r u", b=NB)
                         )
-            for c in range(4):
-                tpb = bank([P, 4, P], BF16, "ob")
-                for i in range(4):
-                    nc.tensor.transpose(tpb[:, i, :], tab2[:, 4 * c + i, :], identb[:])
-                nc.scalar.copy(out=tabT[:, 512 * c : 512 * (c + 1)], in_=tpb[:].rearrange("p i n -> p (i n)"))
-            for c in range(4):
-                pm = bank([P, 2, 512], BF16, "ob")
-                for v, sel in enumerate((sel_c[FIXB], sel_s[FIXB])):
-                    nc.tensor.matmul(out=pm[:, v, :], lhsT=sel[:], rhs=tabT[:, 512 * c : 512 * (c + 1)], start=True, stop=True)
-                nc.scalar.copy(out=cst[FIXB][:, :, 512 * c : 512 * (c + 1)], in_=pm[:])
-            for i, t in enumerate(B3_TILES):
-                pm = bank([P, 2, P], BF16, "ob")
-                for v, sel in enumerate((sel_c[FLEX], sel_s[FLEX])):
-                    nc.tensor.matmul(out=pm[:, v, :], lhsT=sel[:], rhs=tabT[:, P * t : P * (t + 1)], start=True, stop=True)
-                nc.scalar.copy(out=cst[FLEX][:, :, P * i : P * (i + 1)], in_=pm[:])
             for b in (3, 2, 0, 1):
                 for g in range(NG):
                     nc.vector.quantize_mx(
@@ -194,9 +235,9 @@ def tile_attention_pa_kernel(tc, x_bytes, x_scale, freqs_cos, freqs_sin, wq, wk,
                         scales=ws[:, g, 512 * b : 512 * (b + 1)],
                         in_=wg[g][:, b, :, :, :].rearrange("p h r u -> p (h r u)").bitcast(BF16),
                     )
-            x_quant(3)
-            nc.scalar.copy(out=cosf[:], in_=cosb[:, :, 0:32])
-            nc.scalar.activation(out=sgn[:, 0, :, :], in_=sgn[:, 1, :, :], func=ACT.Copy, scale=-1.0)
+            for c in range(4):
+                if c not in XQ_INLINE:
+                    x_quant(c)
 
         mpool = ctx.enter_context(tc.tile_pool(name="mpool", bufs=4))
         opool = ctx.enter_context(tc.tile_pool(name="opool", bufs=4))
@@ -232,13 +273,25 @@ def tile_attention_pa_kernel(tc, x_bytes, x_scale, freqs_cos, freqs_sin, wq, wk,
                 )
             return acc
 
+        def jv(t):
+            return JV_LAST if t == NT - 1 else JV
+
         def a_m1(t, i, acc, m1):
             b = A_FB[i]
             accv = acc[:].rearrange("p (h e j) -> p h e j", h=NH, e=2)
-            for j in range(16):
+            for j in range(16 - jv(t)):
                 nc.scalar.activation(
                     out=m1[:, i, j, :, :], in_=accv[:, :, :, j], func=ACT.Copy, scale=cosf[:, t, 16 * b + j : 16 * b + j + 1]
                 )
+
+        def a_m1v(t, i, acc, m1):
+            b = A_FB[i]
+            nc.vector.tensor_tensor(
+                out=m1[:, i, 16 - jv(t) : 16, :, :].rearrange("p j h e -> p j (h e)"),
+                in0=acc[:].rearrange("p (x j) -> p j x", j=16)[:, 16 - jv(t) : 16, :],
+                in1=cosb[:, t, 16 * b + 16 - jv(t) : 16 * (b + 1)].unsqueeze(2).to_broadcast([P, jv(t), 32]),
+                op=ALU.mult,
+            )
 
         def av_m1(t, b, acc, m1):
             nc.vector.tensor_tensor(
@@ -337,7 +390,8 @@ def tile_attention_pa_kernel(tc, x_bytes, x_scale, freqs_cos, freqs_sin, wq, wk,
             if early_fin:
                 for b in kinds(t - 1)[2]:
                     b_fin(t - 1, b, prods[b])
-                store(t - 1)
+                if t - 1 < VADD_FROM:
+                    store(t - 1)
             if a_list:
                 m1 = mpool.tile([P, 3, 16, NH, 2], F32, name="m1", tag="m1", bufs=3)
                 for i, b in enumerate(a_list):
@@ -362,6 +416,9 @@ def tile_attention_pa_kernel(tc, x_bytes, x_scale, freqs_cos, freqs_sin, wq, wk,
             if t == NT - 1:
                 for b in b_list:
                     b_fin(t, b, prods[b])
+                if LATE_EARLY:
+                    for tl in range(VADD_FROM, NT - 1):
+                        last_adds(tl, late[tl][0], late[tl][1])
             if XPOS == 1 and xp < NT:
                 x_prod(xp)
             for na in next_a[0:1]:
@@ -370,6 +427,8 @@ def tile_attention_pa_kernel(tc, x_bytes, x_scale, freqs_cos, freqs_sin, wq, wk,
                 if b in v_list:
                     av_m1(t, b, accs[(t, b)], m1)
                 a_m2(t, b, accs[(t, b)])
+                if jv(t) and b in a_list:
+                    a_m1v(t, a_list.index(b), accs[(t, b)], m1)
                 for na in next_a[i + 1 : i + 2]:
                     accs[(t + 1, na)] = a_mx(t + 1, na)
             if XPOS == 2 and xp < NT:
@@ -380,7 +439,7 @@ def tile_attention_pa_kernel(tc, x_bytes, x_scale, freqs_cos, freqs_sin, wq, wk,
             else:
                 a_add(t, A_FB[0], n_b, m1[:, 0:n_b, :, :, :].rearrange("p i j h e -> p h (i j) e"))
             if t == NT - 1:
-                for tl in range(VADD_FROM, NT):
+                for tl in range(NT - 1 if LATE_EARLY else VADD_FROM, NT):
                     last_adds(tl, late[tl][0], late[tl][1])
             if XPOS == 3 and xp < NT:
                 x_prod(xp)

@@ -31,7 +31,7 @@ NX_HEAD = 16
 X_BEFORE_W = {3: 1, 8: 2, 13: 3}
 GROUPS = (2, 2, 2, 2, 2, 2, 1, 1, 1, 1)
 XPOS = 0
-TAB_OB = True
+TAB_OB = False
 PE_SCALE = True
 NCHUNK = 2
 LATE_EARLY = False
@@ -68,16 +68,16 @@ def tile_attention_pa_kernel(tc, x_bytes, x_scale, freqs_cos, freqs_sin, wq, wk,
         scale_bc = const.tile([P, D], F32, name="scale_bc")
         cosb = const.tile([P, NT, 64], BF16, name="cosb")
         sgn = const.tile([P, 2, NT, 64], BF16, name="sgn")
-        tab2 = const.tile([P, NT, P], BF16, name="tab2")
         cosf = const.tile([P, NT, 32], F32, name="cosf")
-        tabT = const.tile([P, NT * P], BF16, name="tabT")
+        tabT = const.tile([P, 2, 8 * P], BF16, name="tabT")
         cst = {}
         sel_c = {}
         sel_s = {}
         for b in B_FB:
             cst[b] = const.tile([P, 2, (NT if b == FIXB else len(B3_TILES)) * P], BF16, name="cst%d" % b)
-            sel_c[b] = const.tile([P, P], BF16, name="selc%d" % b)
-            sel_s[b] = const.tile([P, P], BF16, name="sels%d" % b)
+            for par in range(2):
+                sel_c[(b, par)] = const.tile([P, P], BF16, name="selc%d_%d" % (b, par))
+                sel_s[(b, par)] = const.tile([P, P], BF16, name="sels%d_%d" % (b, par))
         wc = const.tile([P, NG, NB * 512], U32, name="wc", align_bytes=64)
         ws = const.tile([P, NG, NB * 512], U8, name="ws", align_bytes=64)
         xc = const.tile([P, NG, NT * P], U32, name="xc", align_bytes=64)
@@ -159,8 +159,6 @@ def tile_attention_pa_kernel(tc, x_bytes, x_scale, freqs_cos, freqs_sin, wq, wk,
                     nc.sync.dma_start(out=s8[0:8, :], in_=x_scale.rearrange("a b (c n) -> (a b c) n", n=P))
                 elif kind == "s":
                     nc.sync.dma_start(out=scale_bc[:], in_=x_scale.rearrange("a b k -> (a b k)").partition_broadcast(P))
-            nc.sync.dma_start(out=tab2[:, :, 0:64], in_=sin_view)
-            nc.sync.dma_start(out=tab2[:, :, 64:128], in_=cos_view)
             nc.sync.dma_start(out=cosb[:], in_=cos_view)
             nc.sync.dma_start(out=sgn[:, 1, :, :], in_=sin_view)
 
@@ -179,14 +177,13 @@ def tile_attention_pa_kernel(tc, x_bytes, x_scale, freqs_cos, freqs_sin, wq, wk,
                 in_=ident[:].rearrange("p (b e j) -> p b j e", b=NB, e=2)[:, :, :, ::-1],
             )
             for b in B_FB:
-                nc.vector.tensor_copy(
-                    out=sel_c[b][:].rearrange("p (x j) -> p x j", j=16),
-                    in_=identb[:, 64 + 16 * b : 64 + 16 * (b + 1)].unsqueeze(1).to_broadcast([P, 8, 16]),
-                )
-                sv = sel_s[b][:].rearrange("p (h e j) -> p h e j", h=4, e=2)
-                src = identb[:, 16 * b : 16 * (b + 1)].unsqueeze(1).to_broadcast([P, 4, 16])
-                nc.vector.tensor_copy(out=sv[:, :, 0, :], in_=src)
-                nc.vector.tensor_scalar(out=sv[:, :, 1, :], in0=src, scalar1=-1.0, scalar2=None, op0=ALU.mult)
+                for par in range(2):
+                    src8 = identb[:, 64 * par + 16 * b : 64 * par + 16 * (b + 1)].unsqueeze(1).to_broadcast([P, 8, 16])
+                    src4 = identb[:, 64 * par + 16 * b : 64 * par + 16 * (b + 1)].unsqueeze(1).to_broadcast([P, 4, 16])
+                    nc.vector.tensor_copy(out=sel_c[(b, par)][:].rearrange("p (x j) -> p x j", j=16), in_=src8)
+                    sv = sel_s[(b, par)][:].rearrange("p (h e j) -> p h e j", h=4, e=2)
+                    nc.vector.tensor_copy(out=sv[:, :, 0, :], in_=src4)
+                    nc.vector.tensor_scalar(out=sv[:, :, 1, :], in0=src4, scalar1=-1.0, scalar2=None, op0=ALU.mult)
 
             if PE_SCALE:
                 tp0 = tp_bank([P, P], F32)
@@ -208,19 +205,27 @@ def tile_attention_pa_kernel(tc, x_bytes, x_scale, freqs_cos, freqs_sin, wq, wk,
                     nc.scalar.copy(out=cosf[:], in_=cosb[:, :, 0:32])
                     nc.scalar.activation(out=sgn[:, 0, :, :], in_=sgn[:, 1, :, :], func=ACT.Copy, scale=-1.0)
                 elif kind == "tt":
+                    v, half = t // 2, t % 2
+                    src_tab = cosb if v == 0 else sgn[:, 1, :, :]
                     tpb = tab_bank([P, 4, P], BF16)
                     for i in range(4):
-                        nc.tensor.transpose(tpb[:, i, :], tab2[:, 4 * t + i, :], identb[:])
-                    nc.scalar.copy(out=tabT[:, 512 * t : 512 * (t + 1)], in_=tpb[:].rearrange("p i n -> p (i n)"))
+                        pair = 4 * half + i
+                        nc.tensor.transpose(tpb[:, i, :], src_tab[:, 2 * pair : 2 * pair + 2, :].rearrange("p t j -> p (t j)"), identb[:])
+                    nc.scalar.copy(out=tabT[:, v, 512 * half : 512 * (half + 1)], in_=tpb[:].rearrange("p i n -> p (i n)"))
                 elif kind == "ts":
+                    half, par = t // 2, t % 2
                     pm = tab_bank([P, 2, 512], BF16)
-                    for v, sel in enumerate((sel_c[FIXB], sel_s[FIXB])):
-                        nc.tensor.matmul(out=pm[:, v, :], lhsT=sel[:], rhs=tabT[:, 512 * t : 512 * (t + 1)], start=True, stop=True)
-                    nc.scalar.copy(out=cst[FIXB][:, :, 512 * t : 512 * (t + 1)], in_=pm[:])
+                    for v, sel in enumerate((sel_c[(FIXB, par)], sel_s[(FIXB, par)])):
+                        nc.tensor.matmul(out=pm[:, v, :], lhsT=sel[:], rhs=tabT[:, v, 512 * half : 512 * (half + 1)], start=True, stop=True)
+                    nc.scalar.copy(
+                        out=cst[FIXB][:].rearrange("p v (t n) -> p v t n", n=P)[:, :, 8 * half + par : 8 * half + 8 : 2, :],
+                        in_=pm[:].rearrange("p v (i n) -> p v i n", n=P),
+                    )
                 elif kind == "tf":
+                    tile = B3_TILES[t]
                     pm = tab_bank([P, 2, P], BF16)
-                    for v, sel in enumerate((sel_c[FLEX], sel_s[FLEX])):
-                        nc.tensor.matmul(out=pm[:, v, :], lhsT=sel[:], rhs=tabT[:, P * B3_TILES[t] : P * (B3_TILES[t] + 1)], start=True, stop=True)
+                    for v, sel in enumerate((sel_c[(FLEX, tile % 2)], sel_s[(FLEX, tile % 2)])):
+                        nc.tensor.matmul(out=pm[:, v, :], lhsT=sel[:], rhs=tabT[:, v, P * (tile // 2) : P * (tile // 2 + 1)], start=True, stop=True)
                     nc.scalar.copy(out=cst[FLEX][:, :, P * t : P * (t + 1)], in_=pm[:])
                 else:
                     tp = transposes(wraw[t][:].bitcast(F32), perm_w, None)

@@ -20,27 +20,14 @@ NT = 16
 NH = 16
 NB = 4
 NG = 2
-A_FB = (0, 1)
-B3_TILES = (3, 7, 11, 15)
-FLEX = 2
-FIXB = 3
-B_FB = (FIXB, FLEX) if B3_TILES else (FIXB,)
 TP_TAGS = ("acc", "pt", "ob", "acc", "pt", "ob", "acc", "acc")
 TAG_BUFS = {"acc": 4, "pt": 2, "ob": 2}
-NX_HEAD = 16
-X_BEFORE_W = {3: 1, 8: 2, 13: 3}
 GROUPS = (2, 2, 2, 2, 2, 2, 1, 1, 1, 1)
-XPOS = 0
-TAB_OB = False
-PE_SCALE = True
-NCHUNK = 2
-LATE_EARLY = False
-JV_LAST = 0
-XQ_INLINE = (0, 1, 2)
-JV = 0
+B2_TILES = (3, 7, 11, 15)
+B_TILES = {3: tuple(range(NT)), 2: B2_TILES}
 VADD_FROM = 14
-LOADS = (("s8", 0), ("x0", 0), ("w", 0), ("w", 1), ("x0r", 0), ("w", 2), ("w", 3), ("x", 1), ("w", 4), ("w", 5), ("w", 6), ("w", 7), ("w", 8), ("x", 2), ("w", 9), ("w", 10), ("w", 11), ("w", 12), ("x", 3), ("w", 13), ("w", 14), ("w", 15))
-HEAD_ORDER = (("w", 0), ("w", 1), ("x", 0), ("w", 2), ("x", 1), ("w", 3), ("x", 2), ("w", 4), ("x", 3), ("w", 5), ("x", 4), ("w", 6), ("x", 5), ("w", 7), ("x", 6), ("w", 8), ("x", 7), ("w", 9), ("x", 8), ("w", 10), ("x", 9), ("w", 11), ("x", 10), ("w", 12), ("x", 11), ("w", 13), ("x", 12), ("w", 14), ("x", 13), ("w", 15), ("x", 14), ("x", 15), ("tt", 0), ("tt", 1), ("tt", 2), ("tt", 3), ("ts", 0), ("ts", 1), ("ts", 2), ("ts", 3), ("tf", 0), ("tf", 1), ("tf", 2), ("tf", 3), ("cs", 0))
+W_MM = (0, 2, 4, 6, 8, 10, 12, 14)
+X_MM = (1, 3, 5, 7, 9, 11, 13, 15)
 
 
 def tile_attention_pa_kernel(tc, x_bytes, x_scale, freqs_cos, freqs_sin, wq, wk, out_0, out_1):
@@ -49,23 +36,16 @@ def tile_attention_pa_kernel(tc, x_bytes, x_scale, freqs_cos, freqs_sin, wq, wk,
         ctx.enter_context(tc.manual_schedule())
         const = ctx.enter_context(tc.tile_pool(name="const", bufs=1))
         psum = ctx.enter_context(tc.psum_pool(name="psum", bufs=2))
-        head = ExitStack()
-        xin = head.enter_context(tc.tile_pool(name="xin", bufs=1))
-        xwork = head.enter_context(tc.tile_pool(name="xwork", bufs=4))
         counters = {"tp": 0}
 
         def bank(shape, dtype, tag):
             return psum.tile(shape, dtype, name=tag, tag=tag, bufs=TAG_BUFS[tag])
 
-        def tp_bank(shape, dtype):
-            tag = TP_TAGS[counters["tp"] % 8]
+        def any_bank(shape, dtype):
+            tag = TP_TAGS[counters["tp"] % len(TP_TAGS)]
             counters["tp"] += 1
             return bank(shape, dtype, tag)
 
-        def tab_bank(shape, dtype):
-            return bank(shape, dtype, "ob") if TAB_OB else tp_bank(shape, dtype)
-
-        scale_bc = const.tile([P, D], F32, name="scale_bc")
         cosb = const.tile([P, NT, 64], BF16, name="cosb")
         sgn = const.tile([P, 2, NT, 64], BF16, name="sgn")
         cosf = const.tile([P, NT, 32], F32, name="cosf")
@@ -73,9 +53,9 @@ def tile_attention_pa_kernel(tc, x_bytes, x_scale, freqs_cos, freqs_sin, wq, wk,
         cst = {}
         sel_c = {}
         sel_s = {}
-        for b in B_FB:
-            cst[b] = const.tile([P, 2, (NT if b == FIXB else len(B3_TILES)) * P], BF16, name="cst%d" % b)
-            for par in range(2):
+        for b, tiles in B_TILES.items():
+            cst[b] = const.tile([P, 2, len(tiles) * P], BF16, name="cst%d" % b)
+            for par in sorted(set([t % 2 for t in tiles])):
                 sel_c[(b, par)] = const.tile([P, P], BF16, name="selc%d_%d" % (b, par))
                 sel_s[(b, par)] = const.tile([P, P], BF16, name="sels%d_%d" % (b, par))
         wc = const.tile([P, NG, NB * 512], U32, name="wc", align_bytes=64)
@@ -85,80 +65,70 @@ def tile_attention_pa_kernel(tc, x_bytes, x_scale, freqs_cos, freqs_sin, wq, wk,
         ident = const.tile([P, P], F32, name="ident")
         identb = const.tile([P, P], BF16, name="identb")
         perm_w = const.tile([P, P], F32, name="perm_w")
+        perm_wb = const.tile([P, P], BF16, name="perm_wb")
         perm_a = const.tile([P, P], F32, name="perm_a")
         perm_b = const.tile([P, P], F32, name="perm_b")
-        xbytes = [xin.tile([P, 4, D], U8, name="xbytes%d" % c) for c in range(4)]
         x_view = x_bytes.rearrange("o (p t) k -> (o p) t k", t=NT)
         cos_view = freqs_cos.rearrange("(p t) j -> p t j", t=NT)
         sin_view = freqs_sin.rearrange("(p t) j -> p t j", t=NT)
-        xbf = {}
-        xg = {}
 
-        def transposes(words, permutation, tag):
-            tp = bank([P, 4, P], F32, tag) if tag else tp_bank([P, 4, P], F32)
+        def word_transposes(rows, permutation):
+            tp = any_bank([P, 2 * NG, P], F32)
+            words = rows[:].bitcast(F32)
             for g in range(NG):
                 for u in range(2):
                     nc.tensor.transpose(tp[:, 2 * g + u, :], words[:, 256 * g + u : 256 * (g + 1) : 2], permutation[:])
             return tp
 
-        def x_prod(t):
-            xb = xwork.tile([P, D], BF16, name="xbf", tag="xbf", bufs=16)
-            n_c = NCHUNK if t == 0 else 1
-            w_c = D // n_c
-            for c in range(n_c):
-                nc.vector.tensor_tensor(
-                    out=xb[:, w_c * c : w_c * (c + 1)],
-                    in0=xbytes[t // 4][:, t % 4, w_c * c : w_c * (c + 1)].bitcast(FP8),
-                    in1=scale_bc[:, w_c * c : w_c * (c + 1)],
-                    op=ALU.mult,
-                )
-            xbf[t] = xb
-
-        def x_tr(t, tag):
-            if t % 4 == 0:
-                xg[t // 4] = xwork.tile([P, NG, 4, P, 2], F32, name="xg", tag="xg", align_bytes=64)
-            tp = transposes(xbf[t][:].bitcast(F32), ident, tag)
-            nc.scalar.copy(out=xg[t // 4][:, :, t % 4, :, :], in_=tp[:].rearrange("p (g u) n -> p g n u", u=2))
-
-        def x_quant(c):
+        def matmul_transposes(rows, permutation):
+            tp = any_bank([P, NG, 4, P], BF16)
             for g in range(NG):
-                nc.vector.quantize_mx(
-                    out=xc[:, g, 512 * c : 512 * (c + 1)].bitcast(FP8X4),
-                    scales=xs[:, g, 512 * c : 512 * (c + 1)],
-                    in_=xg[c][:, g, :, :, :].rearrange("p a n u -> p (a n u)").bitcast(BF16),
-                )
+                for v in range(4):
+                    nc.tensor.matmul(
+                        out=tp[:, g, v, :], lhsT=rows[:, 512 * g + v : 512 * (g + 1) : 4], rhs=permutation[:], start=True, stop=True
+                    )
+            return tp
 
-        with head:
+        with ExitStack() as head:
+            xin = head.enter_context(tc.tile_pool(name="xin", bufs=1))
+            xwork = head.enter_context(tc.tile_pool(name="xwork", bufs=4))
             wraw_pool = head.enter_context(tc.tile_pool(name="wraw", bufs=NH))
             wgp = head.enter_context(tc.tile_pool(name="wgp", bufs=1))
-            wg = [wgp.tile([P, NB, NH, 32, 2], F32, name="wg%d" % g, align_bytes=64) for g in range(NG)]
+            scale_bc = xin.tile([P, D], F32, name="scale_bc")
+            sp = xin.tile([P, 2, 4], F32, name="sp")
+            xbytes = [xin.tile([P, 4, D], U8, name="xbytes%d" % c) for c in range(4)]
+            wg = [wgp.tile([P, NB, NH, 32, 4], BF16, name="wg%d" % g, align_bytes=64) for g in range(NG)]
             wraw = []
+            xbf = {}
+            xg = {}
 
-            s8 = wgp.tile([P, P], F32, name="s8")
-            sp = wgp.tile([P, 8], F32, name="sp")
-            if PE_SCALE:
-                nc.vector.memset(s8[:], 0.0)
             for h in range(NH):
                 wraw.append(wraw_pool.tile([P, D], BF16, name="wr", tag="wr"))
-            for kind, i in LOADS:
-                if kind == "w":
-                    w = wq if i < 8 else wk
-                    nc.sync.dma_start(out=wraw[i][:], in_=w[(i % 8) * P : (i % 8 + 1) * P, :])
-                elif kind == "x0":
-                    nc.sync.dma_start(out=xbytes[0][:, 0:1, :], in_=x_view[:, 0:1, :])
-                elif kind == "x0r":
-                    nc.sync.dma_start(out=xbytes[0][:, 1:4, :], in_=x_view[:, 1:4, :])
-                elif kind == "x":
-                    nc.sync.dma_start(out=xbytes[i][:], in_=x_view[:, 4 * i : 4 * i + 4, :])
-                elif kind == "sc":
-                    nc.sync.dma_start(
-                        out=scale_bc[:, 256 * i : 256 * (i + 1)],
-                        in_=x_scale.rearrange("a b k -> (a b k)")[256 * i : 256 * (i + 1)].partition_broadcast(P),
-                    )
-                elif kind == "s8":
-                    nc.sync.dma_start(out=s8[0:8, :], in_=x_scale.rearrange("a b (c n) -> (a b c) n", n=P))
-                elif kind == "s":
-                    nc.sync.dma_start(out=scale_bc[:], in_=x_scale.rearrange("a b k -> (a b k)").partition_broadcast(P))
+
+            def load_w(h):
+                w = wq if h < 8 else wk
+                nc.sync.dma_start(out=wraw[h][:], in_=w[(h % 8) * P : (h % 8 + 1) * P, :])
+
+            def load_x(first, last):
+                c = first // 4
+                nc.sync.dma_start(out=xbytes[c][:, first % 4 : first % 4 + last - first, :], in_=x_view[:, first:last, :])
+
+            nc.sync.dma_start(out=sp[:], in_=x_scale.rearrange("a b (h n c) -> (a b n) h c", h=2, c=4))
+            load_x(0, 1)
+            load_w(0)
+            load_w(1)
+            load_x(1, 4)
+            load_w(2)
+            load_w(3)
+            load_x(4, 8)
+            for h in range(4, 9):
+                load_w(h)
+            load_x(8, 12)
+            for h in range(9, 13):
+                load_w(h)
+            load_x(12, 16)
+            for h in range(13, 16):
+                load_w(h)
             nc.sync.dma_start(out=cosb[:], in_=cos_view)
             nc.sync.dma_start(out=sgn[:, 1, :, :], in_=sin_view)
 
@@ -168,6 +138,7 @@ def tile_attention_pa_kernel(tc, x_bytes, x_scale, freqs_cos, freqs_sin, wq, wk,
                 out=perm_w[:].rearrange("p (b e j) -> p b e j", b=NB, e=2),
                 in_=ident[:].rearrange("p (b j e) -> p b e j", b=NB, e=2),
             )
+            nc.vector.tensor_copy(out=perm_wb[:], in_=perm_w[:])
             nc.vector.tensor_copy(
                 out=perm_a[:].rearrange("p (b j e) -> p b j e", b=NB, e=2),
                 in_=ident[:].rearrange("p (b e j) -> p b j e", b=NB, e=2),
@@ -176,73 +147,110 @@ def tile_attention_pa_kernel(tc, x_bytes, x_scale, freqs_cos, freqs_sin, wq, wk,
                 out=perm_b[:].rearrange("p (b j e) -> p b j e", b=NB, e=2),
                 in_=ident[:].rearrange("p (b e j) -> p b j e", b=NB, e=2)[:, :, :, ::-1],
             )
-            for b in B_FB:
-                for par in range(2):
-                    src8 = identb[:, 64 * par + 16 * b : 64 * par + 16 * (b + 1)].unsqueeze(1).to_broadcast([P, 8, 16])
-                    src4 = identb[:, 64 * par + 16 * b : 64 * par + 16 * (b + 1)].unsqueeze(1).to_broadcast([P, 4, 16])
-                    nc.vector.tensor_copy(out=sel_c[(b, par)][:].rearrange("p (x j) -> p x j", j=16), in_=src8)
-                    sv = sel_s[(b, par)][:].rearrange("p (h e j) -> p h e j", h=4, e=2)
-                    nc.vector.tensor_copy(out=sv[:, :, 0, :], in_=src4)
-                    nc.vector.tensor_scalar(out=sv[:, :, 1, :], in0=src4, scalar1=-1.0, scalar2=None, op0=ALU.mult)
+            for b, par in sel_c:
+                src8 = identb[:, 64 * par + 16 * b : 64 * par + 16 * (b + 1)].unsqueeze(1).to_broadcast([P, 8, 16])
+                src4 = identb[:, 64 * par + 16 * b : 64 * par + 16 * (b + 1)].unsqueeze(1).to_broadcast([P, 4, 16])
+                nc.vector.tensor_copy(out=sel_c[(b, par)][:].rearrange("p (x j) -> p x j", j=16), in_=src8)
+                sv = sel_s[(b, par)][:].rearrange("p (h e j) -> p h e j", h=4, e=2)
+                nc.vector.tensor_copy(out=sv[:, :, 0, :], in_=src4)
+                nc.vector.tensor_scalar(out=sv[:, :, 1, :], in0=src4, scalar1=-1.0, scalar2=None, op0=ALU.mult)
 
-            if PE_SCALE:
-                tp0 = tp_bank([P, P], F32)
-                nc.tensor.transpose(tp0[:], s8[:], ident[:])
-                nc.scalar.copy(out=sp[:], in_=tp0[:, 0:8])
+            for half in range(2):
+                tpb = any_bank([P, 4, P], F32)
+                for c in range(4):
+                    nc.tensor.transpose(tpb[:, c, :], sp[:, half, c : c + 1].to_broadcast([P, P]), ident[:])
+                nc.scalar.copy(
+                    out=scale_bc[:, 512 * half : 512 * (half + 1)].rearrange("p (n c) -> p n c", c=4),
+                    in_=tpb[:].rearrange("p c n -> p n c"),
+                )
+
+            for t in range(NT):
+                xbf[t] = xwork.tile([P, D], BF16, name="xbf", tag="xbf", bufs=NT)
+                n_c = 2 if t == 0 else 1
+                w_c = D // n_c
+                for c in range(n_c):
+                    nc.vector.tensor_tensor(
+                        out=xbf[t][:, w_c * c : w_c * (c + 1)],
+                        in0=xbytes[t // 4][:, t % 4, w_c * c : w_c * (c + 1)].bitcast(FP8),
+                        in1=scale_bc[:, w_c * c : w_c * (c + 1)],
+                        op=ALU.mult,
+                    )
+
+            def x_turn(t):
+                if t % 4 == 0:
+                    xg[t // 4] = xwork.tile([P, NG, 4, P, 4], BF16, name="xg", tag="xg", align_bytes=64)
+                dst = xg[t // 4][:, :, t % 4, :, :]
+                if t in X_MM:
+                    tp = matmul_transposes(xbf[t], identb)
+                    nc.scalar.copy(out=dst, in_=tp[:].rearrange("p g v n -> p g n v"))
+                else:
+                    tp = word_transposes(xbf[t], ident)
+                    nc.scalar.copy(
+                        out=dst.rearrange("p g n v -> p g (n v)").bitcast(F32).rearrange("p g (n u) -> p g n u", u=2),
+                        in_=tp[:].rearrange("p (g u) n -> p g n u", u=2),
+                    )
+
+            def w_turn(h):
+                if h in W_MM:
+                    tp = matmul_transposes(wraw[h], perm_wb)
+                    for g in range(NG):
+                        nc.scalar.copy(out=wg[g][:, :, h, :, :], in_=tp[:, g, :, :].rearrange("p v (b r) -> p b r v", b=NB))
+                else:
+                    tp = word_transposes(wraw[h], perm_w)
+                    for g in range(NG):
+                        nc.scalar.copy(
+                            out=wg[g][:, :, h, :, :].rearrange("p b r v -> p b (r v)").bitcast(F32).rearrange("p b (r u) -> p b r u", u=2),
+                            in_=tp[:, 2 * g : 2 * g + 2, :].rearrange("p u (b r) -> p b r u", b=NB),
+                        )
+
+            def x_quant(c):
+                for g in range(NG):
+                    nc.vector.quantize_mx(
+                        out=xc[:, g, 512 * c : 512 * (c + 1)].bitcast(FP8X4),
+                        scales=xs[:, g, 512 * c : 512 * (c + 1)],
+                        in_=xg[c][:, g, :, :, :].rearrange("p a n v -> p (a n v)"),
+                    )
+
+            w_turn(0)
+            for t in range(NT):
+                if t < NT - 1:
+                    w_turn(t + 1)
+                x_turn(t)
+                if t % 4 == 3 and t < NT - 1:
+                    x_quant(t // 4)
+
+            nc.scalar.copy(out=cosf[:], in_=cosb[:, :, 0:32])
+            nc.scalar.activation(out=sgn[:, 0, :, :], in_=sgn[:, 1, :, :], func=ACT.Copy, scale=-1.0)
+            for v, src_tab in enumerate((cosb[:], sgn[:, 1, :, :])):
                 for half in range(2):
-                    tpb = tp_bank([P, 4, P], F32)
-                    for i in range(4):
-                        nc.tensor.transpose(tpb[:, i, :], sp[:, 4 * half + i : 4 * half + i + 1].to_broadcast([P, P]), ident[:])
-                    nc.scalar.copy(out=scale_bc[:, 512 * half : 512 * (half + 1)], in_=tpb[:].rearrange("p i n -> p (i n)"))
-            for t in range(NX_HEAD):
-                x_prod(t)
-            for kind, t in HEAD_ORDER:
-                if kind == "x":
-                    x_tr(t, None)
-                    if t % 4 == 3 and t // 4 in XQ_INLINE:
-                        x_quant(t // 4)
-                elif kind == "cs":
-                    nc.scalar.copy(out=cosf[:], in_=cosb[:, :, 0:32])
-                    nc.scalar.activation(out=sgn[:, 0, :, :], in_=sgn[:, 1, :, :], func=ACT.Copy, scale=-1.0)
-                elif kind == "tt":
-                    v, half = t // 2, t % 2
-                    src_tab = cosb if v == 0 else sgn[:, 1, :, :]
-                    tpb = tab_bank([P, 4, P], BF16)
+                    tpb = any_bank([P, 4, P], BF16)
                     for i in range(4):
                         pair = 4 * half + i
                         nc.tensor.transpose(tpb[:, i, :], src_tab[:, 2 * pair : 2 * pair + 2, :].rearrange("p t j -> p (t j)"), identb[:])
                     nc.scalar.copy(out=tabT[:, v, 512 * half : 512 * (half + 1)], in_=tpb[:].rearrange("p i n -> p (i n)"))
-                elif kind == "ts":
-                    half, par = t // 2, t % 2
-                    pm = tab_bank([P, 2, 512], BF16)
-                    for v, sel in enumerate((sel_c[(FIXB, par)], sel_s[(FIXB, par)])):
+            for half in range(2):
+                for par in range(2):
+                    pm = any_bank([P, 2, 512], BF16)
+                    for v, sel in enumerate((sel_c[(3, par)], sel_s[(3, par)])):
                         nc.tensor.matmul(out=pm[:, v, :], lhsT=sel[:], rhs=tabT[:, v, 512 * half : 512 * (half + 1)], start=True, stop=True)
                     nc.scalar.copy(
-                        out=cst[FIXB][:].rearrange("p v (t n) -> p v t n", n=P)[:, :, 8 * half + par : 8 * half + 8 : 2, :],
+                        out=cst[3][:].rearrange("p v (t n) -> p v t n", n=P)[:, :, 8 * half + par : 8 * half + 8 : 2, :],
                         in_=pm[:].rearrange("p v (i n) -> p v i n", n=P),
                     )
-                elif kind == "tf":
-                    tile = B3_TILES[t]
-                    pm = tab_bank([P, 2, P], BF16)
-                    for v, sel in enumerate((sel_c[(FLEX, tile % 2)], sel_s[(FLEX, tile % 2)])):
-                        nc.tensor.matmul(out=pm[:, v, :], lhsT=sel[:], rhs=tabT[:, v, P * (tile // 2) : P * (tile // 2 + 1)], start=True, stop=True)
-                    nc.scalar.copy(out=cst[FLEX][:, :, P * t : P * (t + 1)], in_=pm[:])
-                else:
-                    tp = transposes(wraw[t][:].bitcast(F32), perm_w, None)
-                    for g in range(NG):
-                        nc.scalar.copy(
-                            out=wg[g][:, :, t, :, :], in_=tp[:, 2 * g : 2 * g + 2, :].rearrange("p u (b r) -> p b r u", b=NB)
-                        )
+            for i, t in enumerate(B2_TILES):
+                pm = any_bank([P, 2, P], BF16)
+                for v, sel in enumerate((sel_c[(2, t % 2)], sel_s[(2, t % 2)])):
+                    nc.tensor.matmul(out=pm[:, v, :], lhsT=sel[:], rhs=tabT[:, v, P * (t // 2) : P * (t // 2 + 1)], start=True, stop=True)
+                nc.scalar.copy(out=cst[2][:, :, P * i : P * (i + 1)], in_=pm[:])
+
             for b in (3, 2, 0, 1):
                 for g in range(NG):
                     nc.vector.quantize_mx(
                         out=wc[:, g, 512 * b : 512 * (b + 1)].bitcast(FP8X4),
                         scales=ws[:, g, 512 * b : 512 * (b + 1)],
-                        in_=wg[g][:, b, :, :, :].rearrange("p h r u -> p (h r u)").bitcast(BF16),
+                        in_=wg[g][:, b, :, :, :].rearrange("p h r v -> p (h r v)"),
                     )
-            for c in range(4):
-                if c not in XQ_INLINE:
-                    x_quant(c)
+            x_quant(NT // 4 - 1)
 
         mpool = ctx.enter_context(tc.tile_pool(name="mpool", bufs=4))
         opool = ctx.enter_context(tc.tile_pool(name="opool", bufs=4))
@@ -278,35 +286,22 @@ def tile_attention_pa_kernel(tc, x_bytes, x_scale, freqs_cos, freqs_sin, wq, wk,
                 )
             return acc
 
-        def jv(t):
-            return JV_LAST if t == NT - 1 else JV
-
-        def a_m1(t, i, acc, m1):
-            b = A_FB[i]
+        def m1_scalar(t, b, acc, m1):
             accv = acc[:].rearrange("p (h e j) -> p h e j", h=NH, e=2)
-            for j in range(16 - jv(t)):
+            for j in range(16):
                 nc.scalar.activation(
-                    out=m1[:, i, j, :, :], in_=accv[:, :, :, j], func=ACT.Copy, scale=cosf[:, t, 16 * b + j : 16 * b + j + 1]
+                    out=m1[:, b, j, :, :], in_=accv[:, :, :, j], func=ACT.Copy, scale=cosf[:, t, 16 * b + j : 16 * b + j + 1]
                 )
 
-        def a_m1v(t, i, acc, m1):
-            b = A_FB[i]
+        def m1_vector(t, b, acc, m1):
             nc.vector.tensor_tensor(
-                out=m1[:, i, 16 - jv(t) : 16, :, :].rearrange("p j h e -> p j (h e)"),
-                in0=acc[:].rearrange("p (x j) -> p j x", j=16)[:, 16 - jv(t) : 16, :],
-                in1=cosb[:, t, 16 * b + 16 - jv(t) : 16 * (b + 1)].unsqueeze(2).to_broadcast([P, jv(t), 32]),
-                op=ALU.mult,
-            )
-
-        def av_m1(t, b, acc, m1):
-            nc.vector.tensor_tensor(
-                out=m1[:, 2, :, :, :].rearrange("p j h e -> p j (h e)"),
+                out=m1[:, b, :, :, :].rearrange("p j h e -> p j (h e)"),
                 in0=acc[:].rearrange("p (x j) -> p j x", j=16),
                 in1=cosb[:, t, 16 * b : 16 * (b + 1)].unsqueeze(2).to_broadcast([P, 16, 32]),
                 op=ALU.mult,
             )
 
-        def a_m2(t, b, acc):
+        def m2_vector(t, b, acc):
             nc.vector.tensor_tensor(
                 out=ot_slice(t, b, 1).rearrange("p h (j e) -> p h j e", e=2),
                 in0=acc[:].rearrange("p (h e j) -> p h j e", h=NH, e=2)[:, :, :, ::-1],
@@ -314,8 +309,8 @@ def tile_attention_pa_kernel(tc, x_bytes, x_scale, freqs_cos, freqs_sin, wq, wk,
                 op=ALU.mult,
             )
 
-        def a_add(t, b, n_b, m1r):
-            otv = ot_slice(t, b, n_b).rearrange("p h (j e) -> p h j e", e=2)
+        def a_add(t, n_b, m1r):
+            otv = ot_slice(t, 0, n_b).rearrange("p h (j e) -> p h j e", e=2)
             nc.gpsimd.tensor_tensor(out=otv, in0=m1r, in1=otv, op=ALU.add)
 
         def b_mx(t, b):
@@ -333,15 +328,13 @@ def tile_attention_pa_kernel(tc, x_bytes, x_scale, freqs_cos, freqs_sin, wq, wk,
                     )
             return pt
 
-        def tab_col(t, b):
-            return t if b == FIXB else B3_TILES.index(t)
-
         def b_prod(t, b, pt):
+            i = B_TILES[b].index(t)
             pr = mpool.tile([P, 2, 4, P], F32, name="pr", tag="pr")
             nc.vector.tensor_tensor(
                 out=pr[:],
                 in0=pt[:].unsqueeze(1).to_broadcast([P, 2, 4, P]),
-                in1=cst[b][:, :, P * tab_col(t, b) : P * (tab_col(t, b) + 1)].unsqueeze(2).to_broadcast([P, 2, 4, P]),
+                in1=cst[b][:, :, P * i : P * (i + 1)].unsqueeze(2).to_broadcast([P, 2, 4, P]),
                 op=ALU.mult,
             )
             return pr
@@ -364,89 +357,65 @@ def tile_attention_pa_kernel(tc, x_bytes, x_scale, freqs_cos, freqs_sin, wq, wk,
                     store_half(t, v)
 
         def last_adds(t, n_b, m1r):
-            otv = ot_slice(t, A_FB[0], n_b).rearrange("p h (j e) -> p h j e", e=2)
+            otv = ot_slice(t, 0, n_b).rearrange("p h (j e) -> p h j e", e=2)
             for v in range(2):
                 nc.vector.tensor_tensor(
                     out=otv[:, 8 * v : 8 * v + 8, :, :], in0=m1r[:, 8 * v : 8 * v + 8, :, :], in1=otv[:, 8 * v : 8 * v + 8, :, :], op=ALU.add
                 )
                 store_half(t, v)
 
-        def kinds(t):
-            if t >= NT:
-                return ((), (), ())
-            if t in B3_TILES:
-                return (A_FB, (), (FIXB, FLEX))
-            return (A_FB, (FLEX,), (FIXB,))
+        def tensor_bands(t):
+            return [b for b in (3, 2) if t in B_TILES[b]] if t < NT else []
+
+        def token_bands(t):
+            return [b for b in (2, 0, 1) if b < 2 or t not in B2_TILES] if t < NT else []
 
         late = {}
         accs = {}
         pts = {}
         prods = {}
-        for b in kinds(0)[2]:
-            pts[(0, b)] = b_mx(0, b)
-        for b in kinds(0)[1] + kinds(0)[0]:
-            accs[(0, b)] = a_mx(0, b)
+        for b in tensor_bands(0):
+            pts[b] = b_mx(0, b)
+        for b in token_bands(0):
+            accs[b] = a_mx(0, b)
         for t in range(NT):
-            a_list, v_list, b_list = kinds(t)
-            next_b = kinds(t + 1)[2]
-            next_a = kinds(t + 1)[1] + kinds(t + 1)[0]
-            xp = NX_HEAD + t
-            early_fin = t >= 99
-            if early_fin:
-                for b in kinds(t - 1)[2]:
-                    b_fin(t - 1, b, prods[b])
+            cur_pts, cur_accs, cur_prods = pts, accs, prods
+            pts, accs, prods = {}, {}, {}
+            bands_a, bands_b = token_bands(t), tensor_bands(t)
+            next_a, next_b = token_bands(t + 1), tensor_bands(t + 1)
+            n_a = len(bands_a)
+            m1 = mpool.tile([P, 3, 16, NH, 2], F32, name="m1", tag="m1", bufs=3)
+            for b in (0, 1):
+                m1_scalar(t, b, cur_accs[b], m1)
+            if t >= 1:
+                for b in tensor_bands(t - 1):
+                    b_fin(t - 1, b, cur_prods[b])
                 if t - 1 < VADD_FROM:
                     store(t - 1)
-            if a_list:
-                m1 = mpool.tile([P, 3, 16, NH, 2], F32, name="m1", tag="m1", bufs=3)
-                for i, b in enumerate(a_list):
-                    a_m1(t, i, accs[(t, b)], m1)
-            if XPOS == 0 and xp < NT:
-                x_prod(xp)
-            if t >= 1 and not early_fin:
-                for b in kinds(t - 1)[2]:
-                    b_fin(t - 1, b, prods[b])
-                if t - 1 < VADD_FROM:
-                    store(t - 1)
-            if NX_HEAD <= xp - 1 < NT:
-                x_tr(xp - 1, "ob")
-            if NX_HEAD <= xp - 2 < NT and (xp - 2) % 4 == 3:
-                x_quant((xp - 2) // 4)
-            for i, b in enumerate(b_list):
-                prods[b] = b_prod(t, b, pts[(t, b)])
+            for i, b in enumerate(bands_b):
+                prods[b] = b_prod(t, b, cur_pts[b])
                 for nb in next_b[i : i + 1]:
-                    pts[(t + 1, nb)] = b_mx(t + 1, nb)
-            for nb in next_b[len(b_list) :]:
-                pts[(t + 1, nb)] = b_mx(t + 1, nb)
+                    pts[nb] = b_mx(t + 1, nb)
+            for nb in next_b[len(bands_b) :]:
+                pts[nb] = b_mx(t + 1, nb)
             if t == NT - 1:
-                for b in b_list:
+                for b in bands_b:
                     b_fin(t, b, prods[b])
-                if LATE_EARLY:
-                    for tl in range(VADD_FROM, NT - 1):
-                        last_adds(tl, late[tl][0], late[tl][1])
-            if XPOS == 1 and xp < NT:
-                x_prod(xp)
-            for na in next_a[0:1]:
-                accs[(t + 1, na)] = a_mx(t + 1, na)
-            for i, b in enumerate(v_list + a_list):
-                if b in v_list:
-                    av_m1(t, b, accs[(t, b)], m1)
-                a_m2(t, b, accs[(t, b)])
-                if jv(t) and b in a_list:
-                    a_m1v(t, a_list.index(b), accs[(t, b)], m1)
-                for na in next_a[i + 1 : i + 2]:
-                    accs[(t + 1, na)] = a_mx(t + 1, na)
-            if XPOS == 2 and xp < NT:
-                x_prod(xp)
-            n_b = 2 + len(v_list)
+            for nb in next_a[0:1]:
+                accs[nb] = a_mx(t + 1, nb)
+            for i, b in enumerate(bands_a):
+                if b == 2:
+                    m1_vector(t, b, cur_accs[b], m1)
+                m2_vector(t, b, cur_accs[b])
+                for nb in next_a[i + 1 : i + 2]:
+                    accs[nb] = a_mx(t + 1, nb)
+            for nb in next_a[n_a + 1 :]:
+                accs[nb] = a_mx(t + 1, nb)
+            m1r = m1[:, 0:n_a, :, :, :].rearrange("p i j h e -> p h (i j) e")
             if t >= VADD_FROM:
-                late[t] = (n_b, m1[:, 0:n_b, :, :, :].rearrange("p i j h e -> p h (i j) e"))
+                late[t] = (n_a, m1r)
             else:
-                a_add(t, A_FB[0], n_b, m1[:, 0:n_b, :, :, :].rearrange("p i j h e -> p h (i j) e"))
+                a_add(t, n_a, m1r)
             if t == NT - 1:
-                for tl in range(NT - 1 if LATE_EARLY else VADD_FROM, NT):
+                for tl in range(VADD_FROM, NT):
                     last_adds(tl, late[tl][0], late[tl][1])
-            if XPOS == 3 and xp < NT:
-                x_prod(xp)
-            for na in next_a[len(v_list + a_list) + 1 :]:
-                accs[(t + 1, na)] = a_mx(t + 1, na)

@@ -26,8 +26,6 @@ GROUPS = (2, 2, 2, 2, 2, 2, 1, 1, 1, 1)
 B2_TILES = (3, 7, 11, 15)
 B_TILES = {3: tuple(range(NT)), 2: B2_TILES}
 VADD_FROM = 14
-W_MM = (0, 2, 4, 6, 8, 10, 12, 14)
-X_MM = (1, 3, 5, 7, 9, 11, 13, 15)
 
 
 def tile_attention_pa_kernel(tc, x_bytes, x_scale, freqs_cos, freqs_sin, wq, wk, out_0, out_1):
@@ -65,7 +63,6 @@ def tile_attention_pa_kernel(tc, x_bytes, x_scale, freqs_cos, freqs_sin, wq, wk,
         ident = const.tile([P, P], F32, name="ident")
         identb = const.tile([P, P], BF16, name="identb")
         perm_w = const.tile([P, P], F32, name="perm_w")
-        perm_wb = const.tile([P, P], BF16, name="perm_wb")
         perm_a = const.tile([P, P], F32, name="perm_a")
         perm_b = const.tile([P, P], F32, name="perm_b")
         x_view = x_bytes.rearrange("o (p t) k -> (o p) t k", t=NT)
@@ -80,15 +77,6 @@ def tile_attention_pa_kernel(tc, x_bytes, x_scale, freqs_cos, freqs_sin, wq, wk,
                     nc.tensor.transpose(tp[:, 2 * g + u, :], words[:, 256 * g + u : 256 * (g + 1) : 2], permutation[:])
             return tp
 
-        def matmul_transposes(rows, permutation):
-            tp = any_bank([P, NG, 4, P], BF16)
-            for g in range(NG):
-                for v in range(4):
-                    nc.tensor.matmul(
-                        out=tp[:, g, v, :], lhsT=rows[:, 512 * g + v : 512 * (g + 1) : 4], rhs=permutation[:], start=True, stop=True
-                    )
-            return tp
-
         with ExitStack() as head:
             xin = head.enter_context(tc.tile_pool(name="xin", bufs=1))
             xwork = head.enter_context(tc.tile_pool(name="xwork", bufs=4))
@@ -97,7 +85,7 @@ def tile_attention_pa_kernel(tc, x_bytes, x_scale, freqs_cos, freqs_sin, wq, wk,
             scale_bc = xin.tile([P, D], F32, name="scale_bc")
             sp = xin.tile([P, 2, 4], F32, name="sp")
             xbytes = [xin.tile([P, 4, D], U8, name="xbytes%d" % c) for c in range(4)]
-            wg = [wgp.tile([P, NB, NH, 32, 4], BF16, name="wg%d" % g, align_bytes=64) for g in range(NG)]
+            wg = [wgp.tile([P, NB, NH, 32, 2], F32, name="wg%d" % g, align_bytes=64) for g in range(NG)]
             wraw = []
             xbf = {}
             xg = {}
@@ -124,13 +112,15 @@ def tile_attention_pa_kernel(tc, x_bytes, x_scale, freqs_cos, freqs_sin, wq, wk,
             for h in range(4, 9):
                 load_w(h)
             load_x(8, 12)
-            for h in range(9, 13):
-                load_w(h)
+            load_w(9)
+            load_w(10)
+            nc.sync.dma_start(out=cosb[:], in_=cos_view)
+            nc.sync.dma_start(out=sgn[:, 1, :, :], in_=sin_view)
+            load_w(11)
+            load_w(12)
             load_x(12, 16)
             for h in range(13, 16):
                 load_w(h)
-            nc.sync.dma_start(out=cosb[:], in_=cos_view)
-            nc.sync.dma_start(out=sgn[:, 1, :, :], in_=sin_view)
 
             make_identity(nc, ident[:])
             make_identity(nc, identb[:])
@@ -138,7 +128,6 @@ def tile_attention_pa_kernel(tc, x_bytes, x_scale, freqs_cos, freqs_sin, wq, wk,
                 out=perm_w[:].rearrange("p (b e j) -> p b e j", b=NB, e=2),
                 in_=ident[:].rearrange("p (b j e) -> p b e j", b=NB, e=2),
             )
-            nc.vector.tensor_copy(out=perm_wb[:], in_=perm_w[:])
             nc.vector.tensor_copy(
                 out=perm_a[:].rearrange("p (b j e) -> p b j e", b=NB, e=2),
                 in_=ident[:].rearrange("p (b e j) -> p b j e", b=NB, e=2),
@@ -178,37 +167,21 @@ def tile_attention_pa_kernel(tc, x_bytes, x_scale, freqs_cos, freqs_sin, wq, wk,
 
             def x_turn(t):
                 if t % 4 == 0:
-                    xg[t // 4] = xwork.tile([P, NG, 4, P, 4], BF16, name="xg", tag="xg", align_bytes=64)
-                dst = xg[t // 4][:, :, t % 4, :, :]
-                if t in X_MM:
-                    tp = matmul_transposes(xbf[t], identb)
-                    nc.scalar.copy(out=dst, in_=tp[:].rearrange("p g v n -> p g n v"))
-                else:
-                    tp = word_transposes(xbf[t], ident)
-                    nc.scalar.copy(
-                        out=dst.rearrange("p g n v -> p g (n v)").bitcast(F32).rearrange("p g (n u) -> p g n u", u=2),
-                        in_=tp[:].rearrange("p (g u) n -> p g n u", u=2),
-                    )
+                    xg[t // 4] = xwork.tile([P, NG, 4, P, 2], F32, name="xg", tag="xg", align_bytes=64)
+                tp = word_transposes(xbf[t], ident)
+                nc.scalar.copy(out=xg[t // 4][:, :, t % 4, :, :], in_=tp[:].rearrange("p (g u) n -> p g n u", u=2))
 
             def w_turn(h):
-                if h in W_MM:
-                    tp = matmul_transposes(wraw[h], perm_wb)
-                    for g in range(NG):
-                        nc.scalar.copy(out=wg[g][:, :, h, :, :], in_=tp[:, g, :, :].rearrange("p v (b r) -> p b r v", b=NB))
-                else:
-                    tp = word_transposes(wraw[h], perm_w)
-                    for g in range(NG):
-                        nc.scalar.copy(
-                            out=wg[g][:, :, h, :, :].rearrange("p b r v -> p b (r v)").bitcast(F32).rearrange("p b (r u) -> p b r u", u=2),
-                            in_=tp[:, 2 * g : 2 * g + 2, :].rearrange("p u (b r) -> p b r u", b=NB),
-                        )
+                tp = word_transposes(wraw[h], perm_w)
+                for g in range(NG):
+                    nc.scalar.copy(out=wg[g][:, :, h, :, :], in_=tp[:, 2 * g : 2 * g + 2, :].rearrange("p u (b r) -> p b r u", b=NB))
 
             def x_quant(c):
                 for g in range(NG):
                     nc.vector.quantize_mx(
                         out=xc[:, g, 512 * c : 512 * (c + 1)].bitcast(FP8X4),
                         scales=xs[:, g, 512 * c : 512 * (c + 1)],
-                        in_=xg[c][:, g, :, :, :].rearrange("p a n v -> p (a n v)"),
+                        in_=xg[c][:, g, :, :, :].rearrange("p a n u -> p (a n u)").bitcast(BF16),
                     )
 
             w_turn(0)
@@ -216,11 +189,13 @@ def tile_attention_pa_kernel(tc, x_bytes, x_scale, freqs_cos, freqs_sin, wq, wk,
                 if t < NT - 1:
                     w_turn(t + 1)
                 x_turn(t)
+                if t == 9:
+                    nc.scalar.copy(out=cosf[:], in_=cosb[:, :, 0:32])
+                if t == 10:
+                    nc.scalar.activation(out=sgn[:, 0, :, :], in_=sgn[:, 1, :, :], func=ACT.Copy, scale=-1.0)
                 if t % 4 == 3 and t < NT - 1:
                     x_quant(t // 4)
 
-            nc.scalar.copy(out=cosf[:], in_=cosb[:, :, 0:32])
-            nc.scalar.activation(out=sgn[:, 0, :, :], in_=sgn[:, 1, :, :], func=ACT.Copy, scale=-1.0)
             for v, src_tab in enumerate((cosb[:], sgn[:, 1, :, :])):
                 for half in range(2):
                     tpb = any_bank([P, 4, P], BF16)
@@ -248,7 +223,7 @@ def tile_attention_pa_kernel(tc, x_bytes, x_scale, freqs_cos, freqs_sin, wq, wk,
                     nc.vector.quantize_mx(
                         out=wc[:, g, 512 * b : 512 * (b + 1)].bitcast(FP8X4),
                         scales=ws[:, g, 512 * b : 512 * (b + 1)],
-                        in_=wg[g][:, b, :, :, :].rearrange("p h r v -> p (h r v)"),
+                        in_=wg[g][:, b, :, :, :].rearrange("p h r u -> p (h r u)").bitcast(BF16),
                     )
             x_quant(NT // 4 - 1)
 

@@ -23,9 +23,10 @@ NG = 2
 TP_TAGS = ("acc", "pt", "ob", "acc", "pt", "ob", "acc", "acc")
 TAG_BUFS = {"acc": 4, "pt": 2, "ob": 2}
 GROUPS = (2, 2, 2, 2, 2, 2, 1, 1, 1, 1)
-B2_TILES = (3, 7, 11, 15)
+B2_TILES = (3, 7, 11, 14, 15)
 B_TILES = {3: tuple(range(NT)), 2: B2_TILES}
-VADD_FROM = 14
+G_HALVES = (13, 14)
+SP_FLEX = {(t, 1): 15 for t in range(NT)}
 
 
 def tile_attention_pa_kernel(tc, x_bytes, x_scale, freqs_cos, freqs_sin, wq, wk, out_0, out_1):
@@ -83,7 +84,7 @@ def tile_attention_pa_kernel(tc, x_bytes, x_scale, freqs_cos, freqs_sin, wq, wk,
             wraw_pool = head.enter_context(tc.tile_pool(name="wraw", bufs=NH))
             wgp = head.enter_context(tc.tile_pool(name="wgp", bufs=1))
             scale_bc = xin.tile([P, D], F32, name="scale_bc")
-            sp = xin.tile([P, 2, 4], F32, name="sp")
+            sp = xin.tile([P, 4, 2], F32, name="sp")
             xbytes = [xin.tile([P, 4, D], U8, name="xbytes%d" % c) for c in range(4)]
             wg = [wgp.tile([P, NB, NH, 32, 2], F32, name="wg%d" % g, align_bytes=64) for g in range(NG)]
             wraw = []
@@ -101,7 +102,7 @@ def tile_attention_pa_kernel(tc, x_bytes, x_scale, freqs_cos, freqs_sin, wq, wk,
                 c = first // 4
                 nc.sync.dma_start(out=xbytes[c][:, first % 4 : first % 4 + last - first, :], in_=x_view[:, first:last, :])
 
-            nc.sync.dma_start(out=sp[:], in_=x_scale.rearrange("a b (h n c) -> (a b n) h c", h=2, c=4))
+            nc.sync.dma_start(out=sp[:], in_=x_scale.rearrange("a b (q n c) -> (a b n) q c", q=4, c=2))
             load_x(0, 1)
             load_w(0)
             load_w(1)
@@ -144,18 +145,18 @@ def tile_attention_pa_kernel(tc, x_bytes, x_scale, freqs_cos, freqs_sin, wq, wk,
                 nc.vector.tensor_copy(out=sv[:, :, 0, :], in_=src4)
                 nc.vector.tensor_scalar(out=sv[:, :, 1, :], in0=src4, scalar1=-1.0, scalar2=None, op0=ALU.mult)
 
-            for half in range(2):
-                tpb = any_bank([P, 4, P], F32)
-                for c in range(4):
-                    nc.tensor.transpose(tpb[:, c, :], sp[:, half, c : c + 1].to_broadcast([P, P]), ident[:])
+            for q in range(4):
+                tpb = any_bank([P, 2, P], F32)
+                for c in range(2):
+                    nc.tensor.transpose(tpb[:, c, :], sp[:, q, c : c + 1].to_broadcast([P, P]), ident[:])
                 nc.scalar.copy(
-                    out=scale_bc[:, 512 * half : 512 * (half + 1)].rearrange("p (n c) -> p n c", c=4),
+                    out=scale_bc[:, 256 * q : 256 * (q + 1)].rearrange("p (n c) -> p n c", c=2),
                     in_=tpb[:].rearrange("p c n -> p n c"),
                 )
 
             for t in range(NT):
                 xbf[t] = xwork.tile([P, D], BF16, name="xbf", tag="xbf", bufs=NT)
-                n_c = 2 if t == 0 else 1
+                n_c = 4 if t == 0 else 1
                 w_c = D // n_c
                 for c in range(n_c):
                     nc.vector.tensor_tensor(
@@ -263,16 +264,22 @@ def tile_attention_pa_kernel(tc, x_bytes, x_scale, freqs_cos, freqs_sin, wq, wk,
 
         def m1_scalar(t, b, acc, m1):
             accv = acc[:].rearrange("p (h e j) -> p h e j", h=NH, e=2)
-            for j in range(16):
+            for j in range(s_pairs(t, b)):
                 nc.scalar.activation(
                     out=m1[:, b, j, :, :], in_=accv[:, :, :, j], func=ACT.Copy, scale=cosf[:, t, 16 * b + j : 16 * b + j + 1]
                 )
 
+        def s_pairs(t, b):
+            return SP_FLEX.get((t, b), 16 if b < 2 else 0)
+
         def m1_vector(t, b, acc, m1):
+            j0 = s_pairs(t, b)
+            if j0 == 16:
+                return
             nc.vector.tensor_tensor(
-                out=m1[:, b, :, :, :].rearrange("p j h e -> p j (h e)"),
-                in0=acc[:].rearrange("p (x j) -> p j x", j=16),
-                in1=cosb[:, t, 16 * b : 16 * (b + 1)].unsqueeze(2).to_broadcast([P, 16, 32]),
+                out=m1[:, b, j0:16, :, :].rearrange("p j h e -> p j (h e)"),
+                in0=acc[:].rearrange("p (x j) -> p j x", j=16)[:, j0:16, :],
+                in1=cosb[:, t, 16 * b + j0 : 16 * (b + 1)].unsqueeze(2).to_broadcast([P, 16 - j0, 32]),
                 op=ALU.mult,
             )
 
@@ -314,12 +321,17 @@ def tile_attention_pa_kernel(tc, x_bytes, x_scale, freqs_cos, freqs_sin, wq, wk,
             )
             return pr
 
-        def b_fin(t, b, pr):
+        def b_fin(t, b, pr, halves=1):
             ob = bank([P, 4, P], F32, "ob")
             for hq in range(4):
                 nc.tensor.matmul(out=ob[:, hq, :], lhsT=pr[:, 0, hq, :], rhs=perm_a[:], start=True, stop=False, is_transpose=True)
                 nc.tensor.matmul(out=ob[:, hq, :], lhsT=pr[:, 1, hq, :], rhs=perm_b[:], start=False, stop=True, is_transpose=True)
-            nc.scalar.copy(out=ot_slice(t, b, 1), in_=ob[:].rearrange("p q (h r) -> p (q h) r", h=4))
+            for v in range(halves):
+                n_q = 4 // halves
+                nc.scalar.copy(
+                    out=ot_slice(t, b, 1)[:, 4 * n_q * v : 4 * n_q * (v + 1), :],
+                    in_=ob[:, n_q * v : n_q * (v + 1), :].rearrange("p q (h r) -> p (q h) r", h=4),
+                )
 
         def store_half(t, v):
             first, n_t = group_of[t]
@@ -331,13 +343,11 @@ def tile_attention_pa_kernel(tc, x_bytes, x_scale, freqs_cos, freqs_sin, wq, wk,
                 for v in range(2):
                     store_half(t, v)
 
-        def last_adds(t, n_b, m1r):
-            otv = ot_slice(t, 0, n_b).rearrange("p h (j e) -> p h j e", e=2)
-            for v in range(2):
-                nc.vector.tensor_tensor(
-                    out=otv[:, 8 * v : 8 * v + 8, :, :], in0=m1r[:, 8 * v : 8 * v + 8, :, :], in1=otv[:, 8 * v : 8 * v + 8, :, :], op=ALU.add
-                )
-                store_half(t, v)
+        def add_half(engine, t, n_b, m1, v):
+            hs = slice(8 * v, 8 * v + 8)
+            otv = ot_slice(t, 0, n_b).rearrange("p h (j e) -> p h j e", e=2)[:, hs, :, :]
+            m1r = m1[:, 0:n_b, :, :, :].rearrange("p i j h e -> p h (i j) e")[:, hs, :, :]
+            engine.tensor_tensor(out=otv, in0=m1r, in1=otv, op=ALU.add)
 
         def tensor_bands(t):
             return [b for b in (3, 2) if t in B_TILES[b]] if t < NT else []
@@ -345,7 +355,6 @@ def tile_attention_pa_kernel(tc, x_bytes, x_scale, freqs_cos, freqs_sin, wq, wk,
         def token_bands(t):
             return [b for b in (2, 0, 1) if b < 2 or t not in B2_TILES] if t < NT else []
 
-        late = {}
         accs = {}
         pts = {}
         prods = {}
@@ -353,7 +362,7 @@ def tile_attention_pa_kernel(tc, x_bytes, x_scale, freqs_cos, freqs_sin, wq, wk,
             pts[b] = b_mx(0, b)
         for b in token_bands(0):
             accs[b] = a_mx(0, b)
-        for t in range(NT):
+        for t in range(NT - 2):
             cur_pts, cur_accs, cur_prods = pts, accs, prods
             pts, accs, prods = {}, {}, {}
             bands_a, bands_b = token_bands(t), tensor_bands(t)
@@ -365,32 +374,61 @@ def tile_attention_pa_kernel(tc, x_bytes, x_scale, freqs_cos, freqs_sin, wq, wk,
             if t >= 1:
                 for b in tensor_bands(t - 1):
                     b_fin(t - 1, b, cur_prods[b])
-                if t - 1 < VADD_FROM:
-                    store(t - 1)
+                store(t - 1)
             for i, b in enumerate(bands_b):
                 prods[b] = b_prod(t, b, cur_pts[b])
                 for nb in next_b[i : i + 1]:
                     pts[nb] = b_mx(t + 1, nb)
             for nb in next_b[len(bands_b) :]:
                 pts[nb] = b_mx(t + 1, nb)
-            if t == NT - 1:
-                for b in bands_b:
-                    b_fin(t, b, prods[b])
             for nb in next_a[0:1]:
                 accs[nb] = a_mx(t + 1, nb)
             for i, b in enumerate(bands_a):
-                if b == 2:
-                    m1_vector(t, b, cur_accs[b], m1)
+                m1_vector(t, b, cur_accs[b], m1)
                 m2_vector(t, b, cur_accs[b])
                 for nb in next_a[i + 1 : i + 2]:
                     accs[nb] = a_mx(t + 1, nb)
             for nb in next_a[n_a + 1 :]:
                 accs[nb] = a_mx(t + 1, nb)
-            m1r = m1[:, 0:n_a, :, :, :].rearrange("p i j h e -> p h (i j) e")
-            if t >= VADD_FROM:
-                late[t] = (n_a, m1r)
+            if t in G_HALVES:
+                for v in range(2):
+                    add_half(nc.gpsimd, t, n_a, m1, v)
             else:
-                a_add(t, n_a, m1r)
-            if t == NT - 1:
-                for tl in range(VADD_FROM, NT):
-                    last_adds(tl, late[tl][0], late[tl][1])
+                a_add(t, n_a, m1[:, 0:n_a, :, :, :].rearrange("p i j h e -> p h (i j) e"))
+
+        t, u = NT - 2, NT - 1
+        m1s = {}
+
+        def scalar_part(tile, acc):
+            m1s[tile] = mpool.tile([P, 3, 16, NH, 2], F32, name="m1", tag="m1", bufs=3)
+            for b in (0, 1):
+                m1_scalar(tile, b, acc[b], m1s[tile])
+
+        def vector_part(tile, acc):
+            for b in (0, 1):
+                m1_vector(tile, b, acc[b], m1s[tile])
+                m2_vector(tile, b, acc[b])
+
+        scalar_part(t, accs)
+        b_fin(t - 1, 3, prods[3])
+        store(t - 1)
+        pr_t = {3: b_prod(t, 3, pts[3])}
+        pts_u = {3: b_mx(u, 3)}
+        accs_u = {b: a_mx(u, b) for b in (0, 1)}
+        pr_t[2] = b_prod(t, 2, pts[2])
+        pts_u[2] = b_mx(u, 2)
+        vector_part(t, accs)
+        for v in range(2):
+            add_half(nc.gpsimd, t, 2, m1s[t], v)
+        scalar_part(u, accs_u)
+        for b in (3, 2):
+            b_fin(t, b, pr_t[b], 1)
+        store(t)
+        pr_u = {3: b_prod(u, 3, pts_u[3])}
+        pr_u[2] = b_prod(u, 2, pts_u[2])
+        b_fin(u, 3, pr_u[3])
+        b_fin(u, 2, pr_u[2])
+        vector_part(u, accs_u)
+        for v in range(2):
+            add_half(nc.vector, u, 2, m1s[u], v)
+            store_half(u, v)

@@ -26,7 +26,10 @@ GROUPS = (2, 2, 2, 2, 2, 2, 1, 1, 1, 1)
 B2_TILES = (3, 7, 11, 14, 15)
 B_TILES = {3: tuple(range(NT)), 2: B2_TILES}
 G_HALVES = (13, 14)
-SP_FLEX = {(t, 1): 15 for t in range(NT)}
+W_SORTED = ()
+SORT_AHEAD = 2
+SPLIT = (0,)
+SP_FLEX = {}
 
 
 def tile_attention_pa_kernel(tc, x_bytes, x_scale, freqs_cos, freqs_sin, wq, wk, out_0, out_1):
@@ -70,12 +73,13 @@ def tile_attention_pa_kernel(tc, x_bytes, x_scale, freqs_cos, freqs_sin, wq, wk,
         cos_view = freqs_cos.rearrange("(p t) j -> p t j", t=NT)
         sin_view = freqs_sin.rearrange("(p t) j -> p t j", t=NT)
 
-        def word_transposes(rows, permutation):
+        def word_transposes(rows, permutation, in_order=None):
             tp = any_bank([P, 2 * NG, P], F32)
             words = rows[:].bitcast(F32)
             for g in range(NG):
                 for u in range(2):
-                    nc.tensor.transpose(tp[:, 2 * g + u, :], words[:, 256 * g + u : 256 * (g + 1) : 2], permutation[:])
+                    source = in_order[:, 2 * g + u, :] if in_order is not None else words[:, 256 * g + u : 256 * (g + 1) : 2]
+                    nc.tensor.transpose(tp[:, 2 * g + u, :], source, permutation[:])
             return tp
 
         with ExitStack() as head:
@@ -84,7 +88,7 @@ def tile_attention_pa_kernel(tc, x_bytes, x_scale, freqs_cos, freqs_sin, wq, wk,
             wraw_pool = head.enter_context(tc.tile_pool(name="wraw", bufs=NH))
             wgp = head.enter_context(tc.tile_pool(name="wgp", bufs=1))
             scale_bc = xin.tile([P, D], F32, name="scale_bc")
-            sp = xin.tile([P, 4, 2], F32, name="sp")
+            sp = xin.tile([P, 2, 4], F32, name="sp")
             xbytes = [xin.tile([P, 4, D], U8, name="xbytes%d" % c) for c in range(4)]
             wg = [wgp.tile([P, NB, NH, 32, 2], F32, name="wg%d" % g, align_bytes=64) for g in range(NG)]
             wraw = []
@@ -102,7 +106,7 @@ def tile_attention_pa_kernel(tc, x_bytes, x_scale, freqs_cos, freqs_sin, wq, wk,
                 c = first // 4
                 nc.sync.dma_start(out=xbytes[c][:, first % 4 : first % 4 + last - first, :], in_=x_view[:, first:last, :])
 
-            nc.sync.dma_start(out=sp[:], in_=x_scale.rearrange("a b (q n c) -> (a b n) q c", q=4, c=2))
+            nc.sync.dma_start(out=sp[:], in_=x_scale.rearrange("a b (h n c) -> (a b n) h c", h=2, c=4))
             load_x(0, 1)
             load_w(0)
             load_w(1)
@@ -145,18 +149,18 @@ def tile_attention_pa_kernel(tc, x_bytes, x_scale, freqs_cos, freqs_sin, wq, wk,
                 nc.vector.tensor_copy(out=sv[:, :, 0, :], in_=src4)
                 nc.vector.tensor_scalar(out=sv[:, :, 1, :], in0=src4, scalar1=-1.0, scalar2=None, op0=ALU.mult)
 
-            for q in range(4):
-                tpb = any_bank([P, 2, P], F32)
-                for c in range(2):
-                    nc.tensor.transpose(tpb[:, c, :], sp[:, q, c : c + 1].to_broadcast([P, P]), ident[:])
+            for half in range(2):
+                tpb = any_bank([P, 4, P], F32)
+                for c in range(4):
+                    nc.tensor.transpose(tpb[:, c, :], sp[:, half, c : c + 1].to_broadcast([P, P]), ident[:])
                 nc.scalar.copy(
-                    out=scale_bc[:, 256 * q : 256 * (q + 1)].rearrange("p (n c) -> p n c", c=2),
+                    out=scale_bc[:, 512 * half : 512 * (half + 1)].rearrange("p (n c) -> p n c", c=4),
                     in_=tpb[:].rearrange("p c n -> p n c"),
                 )
 
             for t in range(NT):
                 xbf[t] = xwork.tile([P, D], BF16, name="xbf", tag="xbf", bufs=NT)
-                n_c = 4 if t == 0 else 1
+                n_c = 2 if t == 0 else 1
                 w_c = D // n_c
                 for c in range(n_c):
                     nc.vector.tensor_tensor(
@@ -167,26 +171,37 @@ def tile_attention_pa_kernel(tc, x_bytes, x_scale, freqs_cos, freqs_sin, wq, wk,
                     )
 
             def x_turn(t):
-                if t % 4 == 0:
-                    xg[t // 4] = xwork.tile([P, NG, 4, P, 2], F32, name="xg", tag="xg", align_bytes=64)
+                if t % 8 == 0:
+                    xg[t // 8] = xwork.tile([P, NG, 8, P, 2], F32, name="xg", tag="xg", bufs=2, align_bytes=64)
                 tp = word_transposes(xbf[t], ident)
-                nc.scalar.copy(out=xg[t // 4][:, :, t % 4, :, :], in_=tp[:].rearrange("p (g u) n -> p g n u", u=2))
+                nc.scalar.copy(out=xg[t // 8][:, :, t % 8, :, :], in_=tp[:].rearrange("p (g u) n -> p g n u", u=2))
 
             def w_turn(h):
-                tp = word_transposes(wraw[h], perm_w)
+                tp = word_transposes(wraw[h], perm_w, sorted_words.get(h))
                 for g in range(NG):
                     nc.scalar.copy(out=wg[g][:, :, h, :, :], in_=tp[:, 2 * g : 2 * g + 2, :].rearrange("p u (b r) -> p b r u", b=NB))
 
             def x_quant(c):
                 for g in range(NG):
                     nc.vector.quantize_mx(
-                        out=xc[:, g, 512 * c : 512 * (c + 1)].bitcast(FP8X4),
-                        scales=xs[:, g, 512 * c : 512 * (c + 1)],
+                        out=xc[:, g, 1024 * c : 1024 * (c + 1)].bitcast(FP8X4),
+                        scales=xs[:, g, 1024 * c : 1024 * (c + 1)],
                         in_=xg[c][:, g, :, :, :].rearrange("p a n u -> p (a n u)").bitcast(BF16),
                     )
 
+            sorted_words = {}
+
+            def w_sort(h):
+                sorted_words[h] = wgp.tile([P, 2 * NG, P], F32, name="wsort", tag="wsort", bufs=3)
+                nc.scalar.copy(
+                    out=sorted_words[h][:].rearrange("p (g u) q -> p g u q", u=2),
+                    in_=wraw[h][:].bitcast(F32).rearrange("p (g q u) -> p g u q", g=NG, u=2),
+                )
+
             w_turn(0)
             for t in range(NT):
+                if t + 1 + SORT_AHEAD in W_SORTED:
+                    w_sort(t + 1 + SORT_AHEAD)
                 if t < NT - 1:
                     w_turn(t + 1)
                 x_turn(t)
@@ -194,8 +209,8 @@ def tile_attention_pa_kernel(tc, x_bytes, x_scale, freqs_cos, freqs_sin, wq, wk,
                     nc.scalar.copy(out=cosf[:], in_=cosb[:, :, 0:32])
                 if t == 10:
                     nc.scalar.activation(out=sgn[:, 0, :, :], in_=sgn[:, 1, :, :], func=ACT.Copy, scale=-1.0)
-                if t % 4 == 3 and t < NT - 1:
-                    x_quant(t // 4)
+                if t == 7:
+                    x_quant(0)
 
             for v, src_tab in enumerate((cosb[:], sgn[:, 1, :, :])):
                 for half in range(2):
@@ -219,14 +234,14 @@ def tile_attention_pa_kernel(tc, x_bytes, x_scale, freqs_cos, freqs_sin, wq, wk,
                     nc.tensor.matmul(out=pm[:, v, :], lhsT=sel[:], rhs=tabT[:, v, P * (t // 2) : P * (t // 2 + 1)], start=True, stop=True)
                 nc.scalar.copy(out=cst[2][:, :, P * i : P * (i + 1)], in_=pm[:])
 
-            for b in (3, 2, 0, 1):
+            for b in (2, 0):
                 for g in range(NG):
                     nc.vector.quantize_mx(
-                        out=wc[:, g, 512 * b : 512 * (b + 1)].bitcast(FP8X4),
-                        scales=ws[:, g, 512 * b : 512 * (b + 1)],
-                        in_=wg[g][:, b, :, :, :].rearrange("p h r u -> p (h r u)").bitcast(BF16),
+                        out=wc[:, g, 512 * b : 512 * (b + 2)].bitcast(FP8X4),
+                        scales=ws[:, g, 512 * b : 512 * (b + 2)],
+                        in_=wg[g][:, b : b + 2, :, :, :].rearrange("p b h r u -> p (b h r u)").bitcast(BF16),
                     )
-            x_quant(NT // 4 - 1)
+            x_quant(1)
 
         mpool = ctx.enter_context(tc.tile_pool(name="mpool", bufs=4))
         opool = ctx.enter_context(tc.tile_pool(name="opool", bufs=4))
@@ -291,9 +306,9 @@ def tile_attention_pa_kernel(tc, x_bytes, x_scale, freqs_cos, freqs_sin, wq, wk,
                 op=ALU.mult,
             )
 
-        def a_add(t, n_b, m1r):
-            otv = ot_slice(t, 0, n_b).rearrange("p h (j e) -> p h j e", e=2)
-            nc.gpsimd.tensor_tensor(out=otv, in0=m1r, in1=otv, op=ALU.add)
+        def a_add(t, b0, b1, m1):
+            otv = ot_slice(t, b0, b1 - b0).rearrange("p h (j e) -> p h j e", e=2)
+            nc.gpsimd.tensor_tensor(out=otv, in0=m1[:, b0:b1, :, :, :].rearrange("p i j h e -> p h (i j) e"), in1=otv, op=ALU.add)
 
         def b_mx(t, b):
             pt = bank([P, 4, P], F32, "pt")
@@ -333,9 +348,14 @@ def tile_attention_pa_kernel(tc, x_bytes, x_scale, freqs_cos, freqs_sin, wq, wk,
                     in_=ob[:, n_q * v : n_q * (v + 1), :].rearrange("p q (h r) -> p (q h) r", h=4),
                 )
 
-        def store_half(t, v):
+        def store_heads(t, h0, n_h):
             first, n_t = group_of[t]
-            nc.sync.dma_start(out=out_views[v][:, :, first : first + n_t, :], in_=ots[first][:, 8 * v : 8 * v + 8, :, :])
+            nc.sync.dma_start(
+                out=out_views[h0 // 8][:, h0 % 8 : h0 % 8 + n_h, first : first + n_t, :], in_=ots[first][:, h0 : h0 + n_h, :, :]
+            )
+
+        def store_half(t, v):
+            store_heads(t, 8 * v, 8)
 
         def store(t):
             first, n_t = group_of[t]
@@ -344,7 +364,10 @@ def tile_attention_pa_kernel(tc, x_bytes, x_scale, freqs_cos, freqs_sin, wq, wk,
                     store_half(t, v)
 
         def add_half(engine, t, n_b, m1, v):
-            hs = slice(8 * v, 8 * v + 8)
+            add_heads(engine, t, n_b, m1, 8 * v, 8)
+
+        def add_heads(engine, t, n_b, m1, h0, n_h):
+            hs = slice(h0, h0 + n_h)
             otv = ot_slice(t, 0, n_b).rearrange("p h (j e) -> p h j e", e=2)[:, hs, :, :]
             m1r = m1[:, 0:n_b, :, :, :].rearrange("p i j h e -> p h (i j) e")[:, hs, :, :]
             engine.tensor_tensor(out=otv, in0=m1r, in1=otv, op=ALU.add)
@@ -386,6 +409,8 @@ def tile_attention_pa_kernel(tc, x_bytes, x_scale, freqs_cos, freqs_sin, wq, wk,
             for i, b in enumerate(bands_a):
                 m1_vector(t, b, cur_accs[b], m1)
                 m2_vector(t, b, cur_accs[b])
+                if b == 2 and t in SPLIT:
+                    a_add(t, 2, 3, m1)
                 for nb in next_a[i + 1 : i + 2]:
                     accs[nb] = a_mx(t + 1, nb)
             for nb in next_a[n_a + 1 :]:
@@ -394,7 +419,7 @@ def tile_attention_pa_kernel(tc, x_bytes, x_scale, freqs_cos, freqs_sin, wq, wk,
                 for v in range(2):
                     add_half(nc.gpsimd, t, n_a, m1, v)
             else:
-                a_add(t, n_a, m1[:, 0:n_a, :, :, :].rearrange("p i j h e -> p h (i j) e"))
+                a_add(t, 0, 2 if t in SPLIT else n_a, m1)
 
         t, u = NT - 2, NT - 1
         m1s = {}
@@ -429,6 +454,6 @@ def tile_attention_pa_kernel(tc, x_bytes, x_scale, freqs_cos, freqs_sin, wq, wk,
         b_fin(u, 3, pr_u[3])
         b_fin(u, 2, pr_u[2])
         vector_part(u, accs_u)
-        for v in range(2):
-            add_half(nc.vector, u, 2, m1s[u], v)
-            store_half(u, v)
+        for q in range(4):
+            add_heads(nc.vector, u, 2, m1s[u], 4 * q, 4)
+            store_heads(u, 4 * q, 4)

@@ -28,8 +28,11 @@ B_TILES = {3: tuple(range(NT)), 2: B2_TILES}
 G_HALVES = (13, 14)
 W_SORTED = ()
 SORT_AHEAD = 2
+T_HEAD = (("tt", 0), ("tt", 2), ("ts", 0), ("ts", 1), ("tf", 0), ("tf", 1))
+T_NEXT = (("tt", 1), ("tt", 3))
+T_LOOP = {1: ("tf", 2), 2: ("tf", 3), 3: ("tf", 4)}
 SPLIT = (0,)
-SP_FLEX = {}
+SP_FLEX = {(t, 1): 12 for t in B2_TILES}
 
 
 def tile_attention_pa_kernel(tc, x_bytes, x_scale, freqs_cos, freqs_sin, wq, wk, out_0, out_1):
@@ -81,6 +84,31 @@ def tile_attention_pa_kernel(tc, x_bytes, x_scale, freqs_cos, freqs_sin, wq, wk,
                     source = in_order[:, 2 * g + u, :] if in_order is not None else words[:, 256 * g + u : 256 * (g + 1) : 2]
                     nc.tensor.transpose(tp[:, 2 * g + u, :], source, permutation[:])
             return tp
+
+        def table_step(kind, n, get_bank):
+            if kind == "tt":
+                v, half = n // 2, n % 2
+                src_tab = cosb[:] if v == 0 else sgn[:, 1, :, :]
+                tpb = get_bank([P, 4, P], BF16)
+                for i in range(4):
+                    pair = 4 * half + i
+                    nc.tensor.transpose(tpb[:, i, :], src_tab[:, 2 * pair : 2 * pair + 2, :].rearrange("p t j -> p (t j)"), identb[:])
+                nc.scalar.copy(out=tabT[:, v, 512 * half : 512 * (half + 1)], in_=tpb[:].rearrange("p i n -> p (i n)"))
+            elif kind == "ts":
+                half, par = n // 2, n % 2
+                pm = get_bank([P, 2, 512], BF16)
+                for v, sel in enumerate((sel_c[(3, par)], sel_s[(3, par)])):
+                    nc.tensor.matmul(out=pm[:, v, :], lhsT=sel[:], rhs=tabT[:, v, 512 * half : 512 * (half + 1)], start=True, stop=True)
+                nc.scalar.copy(
+                    out=cst[3][:].rearrange("p v (t n) -> p v t n", n=P)[:, :, 8 * half + par : 8 * half + 8 : 2, :],
+                    in_=pm[:].rearrange("p v (i n) -> p v i n", n=P),
+                )
+            else:
+                t = B2_TILES[n]
+                pm = get_bank([P, 2, P], BF16)
+                for v, sel in enumerate((sel_c[(2, t % 2)], sel_s[(2, t % 2)])):
+                    nc.tensor.matmul(out=pm[:, v, :], lhsT=sel[:], rhs=tabT[:, v, P * (t // 2) : P * (t // 2 + 1)], start=True, stop=True)
+                nc.scalar.copy(out=cst[2][:, :, P * n : P * (n + 1)], in_=pm[:])
 
         with ExitStack() as head:
             xin = head.enter_context(tc.tile_pool(name="xin", bufs=1))
@@ -153,14 +181,15 @@ def tile_attention_pa_kernel(tc, x_bytes, x_scale, freqs_cos, freqs_sin, wq, wk,
                 tpb = any_bank([P, 4, P], F32)
                 for c in range(4):
                     nc.tensor.transpose(tpb[:, c, :], sp[:, half, c : c + 1].to_broadcast([P, P]), ident[:])
-                nc.scalar.copy(
-                    out=scale_bc[:, 512 * half : 512 * (half + 1)].rearrange("p (n c) -> p n c", c=4),
-                    in_=tpb[:].rearrange("p c n -> p n c"),
-                )
+                for i in range(2):
+                    nc.scalar.copy(
+                        out=scale_bc[:, 512 * half + 256 * i : 512 * half + 256 * (i + 1)].rearrange("p (n c) -> p n c", c=4),
+                        in_=tpb[:, :, 64 * i : 64 * (i + 1)].rearrange("p c n -> p n c"),
+                    )
 
             for t in range(NT):
                 xbf[t] = xwork.tile([P, D], BF16, name="xbf", tag="xbf", bufs=NT)
-                n_c = 2 if t == 0 else 1
+                n_c = 4 if t == 0 else 1
                 w_c = D // n_c
                 for c in range(n_c):
                     nc.vector.tensor_tensor(
@@ -212,27 +241,8 @@ def tile_attention_pa_kernel(tc, x_bytes, x_scale, freqs_cos, freqs_sin, wq, wk,
                 if t == 7:
                     x_quant(0)
 
-            for v, src_tab in enumerate((cosb[:], sgn[:, 1, :, :])):
-                for half in range(2):
-                    tpb = any_bank([P, 4, P], BF16)
-                    for i in range(4):
-                        pair = 4 * half + i
-                        nc.tensor.transpose(tpb[:, i, :], src_tab[:, 2 * pair : 2 * pair + 2, :].rearrange("p t j -> p (t j)"), identb[:])
-                    nc.scalar.copy(out=tabT[:, v, 512 * half : 512 * (half + 1)], in_=tpb[:].rearrange("p i n -> p (i n)"))
-            for half in range(2):
-                for par in range(2):
-                    pm = any_bank([P, 2, 512], BF16)
-                    for v, sel in enumerate((sel_c[(3, par)], sel_s[(3, par)])):
-                        nc.tensor.matmul(out=pm[:, v, :], lhsT=sel[:], rhs=tabT[:, v, 512 * half : 512 * (half + 1)], start=True, stop=True)
-                    nc.scalar.copy(
-                        out=cst[3][:].rearrange("p v (t n) -> p v t n", n=P)[:, :, 8 * half + par : 8 * half + 8 : 2, :],
-                        in_=pm[:].rearrange("p v (i n) -> p v i n", n=P),
-                    )
-            for i, t in enumerate(B2_TILES):
-                pm = any_bank([P, 2, P], BF16)
-                for v, sel in enumerate((sel_c[(2, t % 2)], sel_s[(2, t % 2)])):
-                    nc.tensor.matmul(out=pm[:, v, :], lhsT=sel[:], rhs=tabT[:, v, P * (t // 2) : P * (t // 2 + 1)], start=True, stop=True)
-                nc.scalar.copy(out=cst[2][:, :, P * i : P * (i + 1)], in_=pm[:])
+            for kind, i in T_HEAD:
+                table_step(kind, i, any_bank)
 
             for b in (2, 0):
                 for g in range(NG):
@@ -381,6 +391,12 @@ def tile_attention_pa_kernel(tc, x_bytes, x_scale, freqs_cos, freqs_sin, wq, wk,
         accs = {}
         pts = {}
         prods = {}
+
+        def ob_bank(shape, dtype):
+            return bank(shape, dtype, "ob")
+
+        for kind, i in T_NEXT:
+            table_step(kind, i, ob_bank)
         for b in tensor_bands(0):
             pts[b] = b_mx(0, b)
         for b in token_bands(0):
@@ -394,10 +410,14 @@ def tile_attention_pa_kernel(tc, x_bytes, x_scale, freqs_cos, freqs_sin, wq, wk,
             m1 = mpool.tile([P, 3, 16, NH, 2], F32, name="m1", tag="m1", bufs=3)
             for b in (0, 1):
                 m1_scalar(t, b, cur_accs[b], m1)
+                if t == 0:
+                    table_step("ts", 2 + b, ob_bank)
             if t >= 1:
                 for b in tensor_bands(t - 1):
                     b_fin(t - 1, b, cur_prods[b])
                 store(t - 1)
+            if t in T_LOOP:
+                table_step(T_LOOP[t][0], T_LOOP[t][1], ob_bank)
             for i, b in enumerate(bands_b):
                 prods[b] = b_prod(t, b, cur_pts[b])
                 for nb in next_b[i : i + 1]:

from contextlib import ExitStack

import concourse.mybir as mybir
from concourse.masks import make_identity

FLOPS = 2 * 2048 * 2048 * 1024

F32 = mybir.dt.float32
BF16 = mybir.dt.bfloat16
U32 = mybir.dt.uint32
U8 = mybir.dt.uint8
FP8 = mybir.dt.float8_e4m3fn
FP8X4 = mybir.dt.float8_e4m3fn_x4
ALU = mybir.AluOpType
ACT = mybir.ActivationFunctionType

P = 128
D = 1024
NT = 16
NH = 16
NB = 4
NG = 2
TP_TAGS = ("acc", "pt", "ob", "acc", "pt", "ob", "acc", "acc")
TAG_BUFS = {"acc": 4, "pt": 2, "ob": 2}
GROUPS = (2, 2, 2, 2, 2, 2, 1, 1, 1, 1)
B2_TILES = (3, 7, 11, 14, 15)
B_TILES = {3: tuple(range(NT)), 2: B2_TILES}
G_HALVES = (13, 14)
W_SORTED = ()
SORT_AHEAD = 2
T_HEAD = (("tt", 0), ("tt", 2), ("ts", 0), ("ts", 1), ("tf", 0), ("tf", 1))
T_NEXT = (("tt", 1), ("tt", 3))
T_LOOP = {1: ("tf", 2), 2: ("tf", 3), 3: ("tf", 4)}
SPLIT = (0,)
SP_FLEX = {(t, 1): 12 for t in B2_TILES}


def tile_attention_pa_kernel(tc, x_bytes, x_scale, freqs_cos, freqs_sin, wq, wk, out_0, out_1):
    nc = tc.nc
    with ExitStack() as ctx:
        ctx.enter_context(tc.manual_schedule())
        const = ctx.enter_context(tc.tile_pool(name="const", bufs=1))
        psum = ctx.enter_context(tc.psum_pool(name="psum", bufs=2))
        counters = {"tp": 0}

        def bank(shape, dtype, tag):
            return psum.tile(shape, dtype, name=tag, tag=tag, bufs=TAG_BUFS[tag])

        def any_bank(shape, dtype):
            tag = TP_TAGS[counters["tp"] % len(TP_TAGS)]
            counters["tp"] += 1
            return bank(shape, dtype, tag)

        cosb = const.tile([P, NT, 64], BF16, name="cosb")
        sgn = const.tile([P, 2, NT, 64], BF16, name="sgn")
        cosf = const.tile([P, NT, 32], F32, name="cosf")
        tabT = const.tile([P, 2, 8 * P], BF16, name="tabT")
        cst = {}
        sel_c = {}
        sel_s = {}
        for b, tiles in B_TILES.items():
            cst[b] = const.tile([P, 2, len(tiles) * P], BF16, name="cst%d" % b)
            for par in sorted(set([t % 2 for t in tiles])):
                sel_c[(b, par)] = const.tile([P, P], BF16, name="selc%d_%d" % (b, par))
                sel_s[(b, par)] = const.tile([P, P], BF16, name="sels%d_%d" % (b, par))
        wc = const.tile([P, NG, NB * 512], U32, name="wc", align_bytes=64)
        ws = const.tile([P, NG, NB * 512], U8, name="ws", align_bytes=64)
        xc = const.tile([P, NG, NT * P], U32, name="xc", align_bytes=64)
        xs = const.tile([P, NG, NT * P], U8, name="xs", align_bytes=64)
        ident = const.tile([P, P], F32, name="ident")
        identb = const.tile([P, P], BF16, name="identb")
        perm_w = const.tile([P, P], F32, name="perm_w")
        perm_a = const.tile([P, P], F32, name="perm_a")
        perm_b = const.tile([P, P], F32, name="perm_b")
        x_view = x_bytes.rearrange("o (p t) k -> (o p) t k", t=NT)
        cos_view = freqs_cos.rearrange("(p t) j -> p t j", t=NT)
        sin_view = freqs_sin.rearrange("(p t) j -> p t j", t=NT)

        def word_transposes(rows, permutation, in_order=None):
            tp = any_bank([P, 2 * NG, P], F32)
            words = rows[:].bitcast(F32)
            for g in range(NG):
                for u in range(2):
                    source = in_order[:, 2 * g + u, :] if in_order is not None else words[:, 256 * g + u : 256 * (g + 1) : 2]
                    nc.tensor.transpose(tp[:, 2 * g + u, :], source, permutation[:])
            return tp

        def table_step(kind, n, get_bank):
            if kind == "tt":
                v, half = n // 2, n % 2
                src_tab = cosb[:] if v == 0 else sgn[:, 1, :, :]
                tpb = get_bank([P, 4, P], BF16)
                for i in range(4):
                    pair = 4 * half + i
                    nc.tensor.transpose(tpb[:, i, :], src_tab[:, 2 * pair : 2 * pair + 2, :].rearrange("p t j -> p (t j)"), identb[:])
                nc.scalar.copy(out=tabT[:, v, 512 * half : 512 * (half + 1)], in_=tpb[:].rearrange("p i n -> p (i n)"))
            elif kind == "ts":
                half, par = n // 2, n % 2
                pm = get_bank([P, 2, 512], BF16)
                for v, sel in enumerate((sel_c[(3, par)], sel_s[(3, par)])):
                    nc.tensor.matmul(out=pm[:, v, :], lhsT=sel[:], rhs=tabT[:, v, 512 * half : 512 * (half + 1)], start=True, stop=True)
                nc.scalar.copy(
                    out=cst[3][:].rearrange("p v (t n) -> p v t n", n=P)[:, :, 8 * half + par : 8 * half + 8 : 2, :],
                    in_=pm[:].rearrange("p v (i n) -> p v i n", n=P),
                )
            else:
                t = B2_TILES[n]
                pm = get_bank([P, 2, P], BF16)
                for v, sel in enumerate((sel_c[(2, t % 2)], sel_s[(2, t % 2)])):
                    nc.tensor.matmul(out=pm[:, v, :], lhsT=sel[:], rhs=tabT[:, v, P * (t // 2) : P * (t // 2 + 1)], start=True, stop=True)
                nc.scalar.copy(out=cst[2][:, :, P * n : P * (n + 1)], in_=pm[:])

        with ExitStack() as head:
            xin = head.enter_context(tc.tile_pool(name="xin", bufs=1))
            xwork = head.enter_context(tc.tile_pool(name="xwork", bufs=4))
            wraw_pool = head.enter_context(tc.tile_pool(name="wraw", bufs=NH))
            wgp = head.enter_context(tc.tile_pool(name="wgp", bufs=1))
            scale_bc = xin.tile([P, D], F32, name="scale_bc")
            sp = xin.tile([P, 2, 4], F32, name="sp")
            xbytes = [xin.tile([P, 4, D], U8, name="xbytes%d" % c) for c in range(4)]
            wg = [wgp.tile([P, NB, NH, 32, 2], F32, name="wg%d" % g, align_bytes=64) for g in range(NG)]
            wraw = []
            xbf = {}
            xg = {}

            for h in range(NH):
                wraw.append(wraw_pool.tile([P, D], BF16, name="wr", tag="wr"))

            def load_w(h):
                w = wq if h < 8 else wk
                nc.sync.dma_start(out=wraw[h][:], in_=w[(h % 8) * P : (h % 8 + 1) * P, :])

            def load_x(first, last):
                c = first // 4
                nc.sync.dma_start(out=xbytes[c][:, first % 4 : first % 4 + last - first, :], in_=x_view[:, first:last, :])

            nc.sync.dma_start(out=sp[:], in_=x_scale.rearrange("a b (h n c) -> (a b n) h c", h=2, c=4))
            load_x(0, 1)
            load_w(0)
            load_w(1)
            load_x(1, 4)
            load_w(2)
            load_w(3)
            load_x(4, 8)
            for h in range(4, 9):
                load_w(h)
            load_x(8, 12)
            load_w(9)
            load_w(10)
            nc.sync.dma_start(out=cosb[:], in_=cos_view)
            nc.sync.dma_start(out=sgn[:, 1, :, :], in_=sin_view)
            load_w(11)
            load_w(12)
            load_x(12, 16)
            for h in range(13, 16):
                load_w(h)

            make_identity(nc, ident[:])
            make_identity(nc, identb[:])
            nc.vector.tensor_copy(
                out=perm_w[:].rearrange("p (b e j) -> p b e j", b=NB, e=2),
                in_=ident[:].rearrange("p (b j e) -> p b e j", b=NB, e=2),
            )
            nc.vector.tensor_copy(
                out=perm_a[:].rearrange("p (b j e) -> p b j e", b=NB, e=2),
                in_=ident[:].rearrange("p (b e j) -> p b j e", b=NB, e=2),
            )
            nc.vector.tensor_copy(
                out=perm_b[:].rearrange("p (b j e) -> p b j e", b=NB, e=2),
                in_=ident[:].rearrange("p (b e j) -> p b j e", b=NB, e=2)[:, :, :, ::-1],
            )
            for b, par in sel_c:
                src8 = identb[:, 64 * par + 16 * b : 64 * par + 16 * (b + 1)].unsqueeze(1).to_broadcast([P, 8, 16])
                src4 = identb[:, 64 * par + 16 * b : 64 * par + 16 * (b + 1)].unsqueeze(1).to_broadcast([P, 4, 16])
                nc.vector.tensor_copy(out=sel_c[(b, par)][:].rearrange("p (x j) -> p x j", j=16), in_=src8)
                sv = sel_s[(b, par)][:].rearrange("p (h e j) -> p h e j", h=4, e=2)
                nc.vector.tensor_copy(out=sv[:, :, 0, :], in_=src4)
                nc.vector.tensor_scalar(out=sv[:, :, 1, :], in0=src4, scalar1=-1.0, scalar2=None, op0=ALU.mult)

            for half in range(2):
                tpb = any_bank([P, 4, P], F32)
                for c in range(4):
                    nc.tensor.transpose(tpb[:, c, :], sp[:, half, c : c + 1].to_broadcast([P, P]), ident[:])
                for i in range(2):
                    nc.scalar.copy(
                        out=scale_bc[:, 512 * half + 256 * i : 512 * half + 256 * (i + 1)].rearrange("p (n c) -> p n c", c=4),
                        in_=tpb[:, :, 64 * i : 64 * (i + 1)].rearrange("p c n -> p n c"),
                    )

            for t in range(NT):
                xbf[t] = xwork.tile([P, D], BF16, name="xbf", tag="xbf", bufs=NT)
                n_c = 4 if t == 0 else 1
                w_c = D // n_c
                for c in range(n_c):
                    nc.vector.tensor_tensor(
                        out=xbf[t][:, w_c * c : w_c * (c + 1)],
                        in0=xbytes[t // 4][:, t % 4, w_c * c : w_c * (c + 1)].bitcast(FP8),
                        in1=scale_bc[:, w_c * c : w_c * (c + 1)],
                        op=ALU.mult,
                    )

            def x_turn(t):
                if t % 8 == 0:
                    xg[t // 8] = xwork.tile([P, NG, 8, P, 2], F32, name="xg", tag="xg", bufs=2, align_bytes=64)
                tp = word_transposes(xbf[t], ident)
                nc.scalar.copy(out=xg[t // 8][:, :, t % 8, :, :], in_=tp[:].rearrange("p (g u) n -> p g n u", u=2))

            def w_turn(h):
                tp = word_transposes(wraw[h], perm_w, sorted_words.get(h))
                for g in range(NG):
                    nc.scalar.copy(out=wg[g][:, :, h, :, :], in_=tp[:, 2 * g : 2 * g + 2, :].rearrange("p u (b r) -> p b r u", b=NB))

            def x_quant(c):
                for g in range(NG):
                    nc.vector.quantize_mx(
                        out=xc[:, g, 1024 * c : 1024 * (c + 1)].bitcast(FP8X4),
                        scales=xs[:, g, 1024 * c : 1024 * (c + 1)],
                        in_=xg[c][:, g, :, :, :].rearrange("p a n u -> p (a n u)").bitcast(BF16),
                    )

            sorted_words = {}

            def w_sort(h):
                sorted_words[h] = wgp.tile([P, 2 * NG, P], F32, name="wsort", tag="wsort", bufs=3)
                nc.scalar.copy(
                    out=sorted_words[h][:].rearrange("p (g u) q -> p g u q", u=2),
                    in_=wraw[h][:].bitcast(F32).rearrange("p (g q u) -> p g u q", g=NG, u=2),
                )

            w_turn(0)
            for t in range(NT):
                if t + 1 + SORT_AHEAD in W_SORTED:
                    w_sort(t + 1 + SORT_AHEAD)
                if t < NT - 1:
                    w_turn(t + 1)
                x_turn(t)
                if t == 9:
                    nc.scalar.copy(out=cosf[:], in_=cosb[:, :, 0:32])
                if t == 10:
                    nc.scalar.activation(out=sgn[:, 0, :, :], in_=sgn[:, 1, :, :], func=ACT.Copy, scale=-1.0)
                if t == 7:
                    x_quant(0)

            for kind, i in T_HEAD:
                table_step(kind, i, any_bank)

            for b in (2, 0):
                for g in range(NG):
                    nc.vector.quantize_mx(
                        out=wc[:, g, 512 * b : 512 * (b + 2)].bitcast(FP8X4),
                        scales=ws[:, g, 512 * b : 512 * (b + 2)],
                        in_=wg[g][:, b : b + 2, :, :, :].rearrange("p b h r u -> p (b h r u)").bitcast(BF16),
                    )
            x_quant(1)

        mpool = ctx.enter_context(tc.tile_pool(name="mpool", bufs=4))
        opool = ctx.enter_context(tc.tile_pool(name="opool", bufs=4))
        out_views = (
            out_0.rearrange("o h (p t) f -> p (o h) t f", t=NT),
            out_1.rearrange("o h (p t) f -> p (o h) t f", t=NT),
        )
        group_of = {}
        t0 = 0
        for n_t in GROUPS:
            for a in range(n_t):
                group_of[t0 + a] = (t0, n_t)
            t0 += n_t
        ots = {}

        def ot_slice(t, b, n_b):
            first, n_t = group_of[t]
            if first not in ots:
                ots[first] = opool.tile([P, NH, n_t, P], F32, name="ot", tag="ot")
            return ots[first][:, :, t - first, 32 * b : 32 * (b + n_b)]

        def a_mx(t, b):
            acc = bank([P, 512], F32, "acc")
            for g in range(NG):
                nc.tensor.matmul_mx(
                    out=acc[:],
                    lhsT=xc[:, g, P * t : P * (t + 1)].bitcast(FP8X4),
                    lhsT_scale=xs[:, g, P * t : P * (t + 1)],
                    rhs=wc[:, g, 512 * b : 512 * (b + 1)].bitcast(FP8X4),
                    rhs_scale=ws[:, g, 512 * b : 512 * (b + 1)],
                    start=(g == 0),
                    stop=(g == NG - 1),
                )
            return acc

        def m1_scalar(t, b, acc, m1):
            accv = acc[:].rearrange("p (h e j) -> p h e j", h=NH, e=2)
            for j in range(s_pairs(t, b)):
                nc.scalar.activation(
                    out=m1[:, b, j, :, :], in_=accv[:, :, :, j], func=ACT.Copy, scale=cosf[:, t, 16 * b + j : 16 * b + j + 1]
                )

        def s_pairs(t, b):
            return SP_FLEX.get((t, b), 16 if b < 2 else 0)

        def m1_vector(t, b, acc, m1):
            j0 = s_pairs(t, b)
            if j0 == 16:
                return
            nc.vector.tensor_tensor(
                out=m1[:, b, j0:16, :, :].rearrange("p j h e -> p j (h e)"),
                in0=acc[:].rearrange("p (x j) -> p j x", j=16)[:, j0:16, :],
                in1=cosb[:, t, 16 * b + j0 : 16 * (b + 1)].unsqueeze(2).to_broadcast([P, 16 - j0, 32]),
                op=ALU.mult,
            )

        def m2_vector(t, b, acc):
            nc.vector.tensor_tensor(
                out=ot_slice(t, b, 1).rearrange("p h (j e) -> p h j e", e=2),
                in0=acc[:].rearrange("p (h e j) -> p h j e", h=NH, e=2)[:, :, :, ::-1],
                in1=sgn[:, :, t, 16 * b : 16 * (b + 1)].rearrange("p e j -> p j e").unsqueeze(1).to_broadcast([P, NH, 16, 2]),
                op=ALU.mult,
            )

        def a_add(t, b0, b1, m1):
            otv = ot_slice(t, b0, b1 - b0).rearrange("p h (j e) -> p h j e", e=2)
            nc.gpsimd.tensor_tensor(out=otv, in0=m1[:, b0:b1, :, :, :].rearrange("p i j h e -> p h (i j) e"), in1=otv, op=ALU.add)

        def b_mx(t, b):
            pt = bank([P, 4, P], F32, "pt")
            for hq in range(4):
                for g in range(NG):
                    nc.tensor.matmul_mx(
                        out=pt[:, hq, :],
                        lhsT=wc[:, g, 512 * b + P * hq : 512 * b + P * (hq + 1)].bitcast(FP8X4),
                        lhsT_scale=ws[:, g, 512 * b + P * hq : 512 * b + P * (hq + 1)],
                        rhs=xc[:, g, P * t : P * (t + 1)].bitcast(FP8X4),
                        rhs_scale=xs[:, g, P * t : P * (t + 1)],
                        start=(g == 0),
                        stop=(g == NG - 1),
                    )
            return pt

        def b_prod(t, b, pt):
            i = B_TILES[b].index(t)
            pr = mpool.tile([P, 2, 4, P], F32, name="pr", tag="pr")
            nc.vector.tensor_tensor(
                out=pr[:],
                in0=pt[:].unsqueeze(1).to_broadcast([P, 2, 4, P]),
                in1=cst[b][:, :, P * i : P * (i + 1)].unsqueeze(2).to_broadcast([P, 2, 4, P]),
                op=ALU.mult,
            )
            return pr

        def b_fin(t, b, pr, halves=1):
            ob = bank([P, 4, P], F32, "ob")
            for hq in range(4):
                nc.tensor.matmul(out=ob[:, hq, :], lhsT=pr[:, 0, hq, :], rhs=perm_a[:], start=True, stop=False, is_transpose=True)
                nc.tensor.matmul(out=ob[:, hq, :], lhsT=pr[:, 1, hq, :], rhs=perm_b[:], start=False, stop=True, is_transpose=True)
            for v in range(halves):
                n_q = 4 // halves
                nc.scalar.copy(
                    out=ot_slice(t, b, 1)[:, 4 * n_q * v : 4 * n_q * (v + 1), :],
                    in_=ob[:, n_q * v : n_q * (v + 1), :].rearrange("p q (h r) -> p (q h) r", h=4),
                )

        def store_heads(t, h0, n_h):
            first, n_t = group_of[t]
            nc.sync.dma_start(
                out=out_views[h0 // 8][:, h0 % 8 : h0 % 8 + n_h, first : first + n_t, :], in_=ots[first][:, h0 : h0 + n_h, :, :]
            )

        def store_half(t, v):
            store_heads(t, 8 * v, 8)

        def store(t):
            first, n_t = group_of[t]
            if t == first + n_t - 1:
                for v in range(2):
                    store_half(t, v)

        def add_half(engine, t, n_b, m1, v):
            add_heads(engine, t, n_b, m1, 8 * v, 8)

        def add_heads(engine, t, n_b, m1, h0, n_h):
            hs = slice(h0, h0 + n_h)
            otv = ot_slice(t, 0, n_b).rearrange("p h (j e) -> p h j e", e=2)[:, hs, :, :]
            m1r = m1[:, 0:n_b, :, :, :].rearrange("p i j h e -> p h (i j) e")[:, hs, :, :]
            engine.tensor_tensor(out=otv, in0=m1r, in1=otv, op=ALU.add)

        def tensor_bands(t):
            return [b for b in (3, 2) if t in B_TILES[b]] if t < NT else []

        def token_bands(t):
            return [b for b in (2, 0, 1) if b < 2 or t not in B2_TILES] if t < NT else []

        accs = {}
        pts = {}
        prods = {}

        def ob_bank(shape, dtype):
            return bank(shape, dtype, "ob")

        for kind, i in T_NEXT:
            table_step(kind, i, ob_bank)
        for b in tensor_bands(0):
            pts[b] = b_mx(0, b)
        for b in token_bands(0):
            accs[b] = a_mx(0, b)
        for t in range(NT - 2):
            cur_pts, cur_accs, cur_prods = pts, accs, prods
            pts, accs, prods = {}, {}, {}
            bands_a, bands_b = token_bands(t), tensor_bands(t)
            next_a, next_b = token_bands(t + 1), tensor_bands(t + 1)
            n_a = len(bands_a)
            m1 = mpool.tile([P, 3, 16, NH, 2], F32, name="m1", tag="m1", bufs=3)
            for b in (0, 1):
                m1_scalar(t, b, cur_accs[b], m1)
                if t == 0:
                    table_step("ts", 2 + b, ob_bank)
            if t >= 1:
                for b in tensor_bands(t - 1):
                    b_fin(t - 1, b, cur_prods[b])
                store(t - 1)
            if t in T_LOOP:
                table_step(T_LOOP[t][0], T_LOOP[t][1], ob_bank)
            for i, b in enumerate(bands_b):
                prods[b] = b_prod(t, b, cur_pts[b])
                for nb in next_b[i : i + 1]:
                    pts[nb] = b_mx(t + 1, nb)
            for nb in next_b[len(bands_b) :]:
                pts[nb] = b_mx(t + 1, nb)
            for nb in next_a[0:1]:
                accs[nb] = a_mx(t + 1, nb)
            for i, b in enumerate(bands_a):
                m1_vector(t, b, cur_accs[b], m1)
                m2_vector(t, b, cur_accs[b])
                if b == 2 and t in SPLIT:
                    a_add(t, 2, 3, m1)
                for nb in next_a[i + 1 : i + 2]:
                    accs[nb] = a_mx(t + 1, nb)
            for nb in next_a[n_a + 1 :]:
                accs[nb] = a_mx(t + 1, nb)
            if t in G_HALVES:
                for v in range(2):
                    add_half(nc.gpsimd, t, n_a, m1, v)
            else:
                a_add(t, 0, 2 if t in SPLIT else n_a, m1)

        t, u = NT - 2, NT - 1
        m1s = {}

        def scalar_part(tile, acc):
            m1s[tile] = mpool.tile([P, 3, 16, NH, 2], F32, name="m1", tag="m1", bufs=3)
            for b in (0, 1):
                m1_scalar(tile, b, acc[b], m1s[tile])

        def vector_part(tile, acc):
            for b in (0, 1):
                m1_vector(tile, b, acc[b], m1s[tile])
                m2_vector(tile, b, acc[b])

        scalar_part(t, accs)
        b_fin(t - 1, 3, prods[3])
        store(t - 1)
        pr_t = {3: b_prod(t, 3, pts[3])}
        pts_u = {3: b_mx(u, 3)}
        accs_u = {b: a_mx(u, b) for b in (0, 1)}
        pr_t[2] = b_prod(t, 2, pts[2])
        pts_u[2] = b_mx(u, 2)
        vector_part(t, accs)
        for v in range(2):
            add_half(nc.gpsimd, t, 2, m1s[t], v)
        scalar_part(u, accs_u)
        for b in (3, 2):
            b_fin(t, b, pr_t[b], 1)
        store(t)
        pr_u = {3: b_prod(u, 3, pts_u[3])}
        pr_u[2] = b_prod(u, 2, pts_u[2])
        b_fin(u, 3, pr_u[3])
        b_fin(u, 2, pr_u[2])
        vector_part(u, accs_u)
        for q in range(4):
            add_heads(nc.vector, u, 2, m1s[u], 4 * q, 4)
            store_heads(u, 4 * q, 4)
